import numpy as np
import ml_dtypes


def mxq(x, axis, fmt="e4m3"):
    dtype, down = {"e4m3": (ml_dtypes.float8_e4m3fn, 7), "e5m2": (ml_dtypes.float8_e5m2, 14)}[fmt]
    v = np.moveaxis(np.asarray(x, np.float32).astype(ml_dtypes.bfloat16).astype(np.float64), axis, -1)
    blocks = v.reshape(v.shape[:-1] + (-1, 32))
    amax = np.abs(blocks).max(-1, keepdims=True)
    byte = np.maximum(np.where(amax > 0, np.frexp(amax)[1] - 1 + 127, 0) - down, 1)
    scale = np.exp2(byte - 127.0)
    codes = (blocks / scale).astype(np.float32).astype(dtype).astype(np.float64)
    return np.moveaxis((codes * scale).reshape(v.shape), -1, axis)


WIDE = False


def mx_kscale(k):
    if not WIDE:
        return np.ones(k)
    levels = np.array([10, -10, 5, -5, 0])
    a = np.random.permutation(np.resize(levels, k // 512 * 4)).reshape(k // 512, 4)
    idx = np.arange(k)
    return np.exp2(a[idx // 512, idx % 128 // 32])


BF16 = ml_dtypes.bfloat16


def bf(x):
    return np.asarray(x, np.float32).astype(BF16)


def f64(x):
    return np.asarray(x).astype(np.float64)


B, I, O, G, P = 4096, 512, 256, 5, 3
GRID_RANGE = (-1.0, 1.0)
L = G + P


def make_grid():
    h = (GRID_RANGE[1] - GRID_RANGE[0]) / G
    n = G + 2 * P + 1
    return np.linspace(GRID_RANGE[0] - P * h, GRID_RANGE[1] + P * h, n)


def b_spline(x, grid, k):
    x = x[..., None]
    g = grid[None, None, :]
    basis = ((x >= g[..., :-1]) & (x < g[..., 1:])).astype(np.float64)
    for p in range(1, k + 1):
        left_denom = g[..., p:-1] - g[..., :-(p + 1)]
        right_denom = g[..., p + 1:] - g[..., 1:-p]
        left_denom = np.where(left_denom > 0, left_denom, np.ones_like(left_denom))
        right_denom = np.where(right_denom > 0, right_denom, np.ones_like(right_denom))
        left = (x - g[..., :-(p + 1)]) / left_denom * basis[..., :-1]
        right = (g[..., p + 1:] - x) / right_denom * basis[..., 1:]
        basis = left + right
    return basis


def setup_inputs():
    s = mx_kscale(I)
    s = s / s.max()
    return {"x": bf(np.random.uniform(-1.0, 1.0, (B, I)) * s),
            "base_weight": bf(np.random.uniform(-1.0, 1.0, (O, I)) * 3.0 / np.sqrt(I) / s),
            "spline_weight": bf(np.random.standard_normal((O, I, L)) * 1.5 / np.sqrt(I))}


def reference(x, base_weight, spline_weight):
    x = f64(x)
    grid = make_grid()
    scale_base, scale_spline = 1.0, 1.0
    base_out = mxq(x, 1, "e4m3") @ mxq(f64(base_weight), 1, "e4m3").T
    basis = b_spline(x, grid, P)
    spline_out = mxq(basis.reshape(B, I * L), 1, "e4m3") @ mxq(f64(spline_weight).reshape(O, I * L), 1, "e4m3").T
    return scale_base * base_out + scale_spline * spline_out

@@ -1,0 +1,180 @@
+from contextlib import ExitStack
+import math
+
+import concourse.bass as bass
+import concourse.mybir as mybir
+import concourse.tile as tile
+from concourse.masks import make_identity
+
+F32 = mybir.dt.float32
+BF16 = mybir.dt.bfloat16
+U32 = mybir.dt.uint32
+U8 = mybir.dt.uint8
+FP8X4 = mybir.dt.float8_e4m3fn_x4
+ALU = mybir.AluOpType
+ACT = mybir.ActivationFunctionType
+
+P = 128
+B, I, O, L = 4096, 512, 256, 8
+NT = B // P
+TPC = 2
+NCH = NT // TPC
+CW = TPC * P * 4
+WW = CW // 4
+FLOPS = 2 * B * O * (I + I * L)
+RS3 = 1.0 / math.sqrt(3.0)
+KNOT = [-2.2 + 0.4 * (t + 4) for t in range(4)]
+
+
+def tile_kanlayer_t_kernel(tc, x, base_weight, spline_weight, out):
+    nc = tc.nc
+    with ExitStack() as ctx:
+        const = ctx.enter_context(tc.tile_pool(name="const", bufs=1))
+        wstage = ctx.enter_context(tc.tile_pool(name="wstage", bufs=2))
+        xgp = ctx.enter_context(tc.tile_pool(name="xgp", bufs=3))
+        f32p = ctx.enter_context(tc.tile_pool(name="f32p", bufs=2))
+        b16p = ctx.enter_context(tc.tile_pool(name="b16p", bufs=2))
+        codep = ctx.enter_context(tc.tile_pool(name="codep", bufs=2))
+        outp = ctx.enter_context(tc.tile_pool(name="outp", bufs=3))
+        ps_x = ctx.enter_context(tc.psum_pool(name="ps_x", bufs=2))
+        ps_w = ctx.enter_context(tc.psum_pool(name="ps_w", bufs=2))
+        ps_o = ctx.enter_context(tc.psum_pool(name="ps_o", bufs=2))
+
+        ident = const.tile([P, P], F32)
+        make_identity(nc, ident[:])
+
+        x_sb = const.tile([P, NT * I], BF16)
+        sw_sb = const.tile([P, 2 * I * L], BF16)
+        bw_sb = const.tile([P, 2 * I], BF16)
+        wc = const.tile([P, 9 * O], U32, align_bytes=64)
+        ws = const.tile([P, 9 * O], U8, align_bytes=64)
+
+        x_v = x.rearrange("(p t) i -> p t i", t=NT)
+        x_t = x_sb[:].rearrange("p (t i) -> p t i", i=I)
+        out_v = out.rearrange("(p t) o -> p t o", t=NT)
+
+        def load_x(j):
+            nc.sync.dma_start(out=x_t[:, 4 * j : 4 * j + 4, :], in_=x_v[:, 4 * j : 4 * j + 4, :])
+
+        load_x(0)
+        nc.sync.dma_start(
+            out=sw_sb[:].rearrange("p (a k) -> p a k", a=2),
+            in_=spline_weight.rearrange("(a p) i l -> p a (i l)", p=P),
+        )
+        nc.sync.dma_start(
+            out=bw_sb[:].rearrange("p (a k) -> p a k", a=2),
+            in_=base_weight.rearrange("(a p) i -> p a i", p=P),
+        )
+        for j in range(1, 8):
+            load_x(j)
+
+        x_w = x_sb[:].bitcast(F32)
+
+        def weights_pass(l):
+            if l < L:
+                wr = wstage.tile([P, 2 * I], BF16)
+                nc.scalar.copy(
+                    out=wr[:].rearrange("p (a i) -> p a i", a=2),
+                    in_=sw_sb[:].rearrange("p (a i l) -> p l a i", a=2, l=L)[:, l],
+                )
+                src = wr
+            else:
+                src = bw_sb
+            src_w = src[:].bitcast(F32)
+            wt = ps_w.tile([P, 2, O], F32)
+            for a in range(2):
+                for u in range(2):
+                    nc.tensor.transpose(
+                        wt[:, u, a * P : (a + 1) * P],
+                        src_w[:, a * 256 + u * P : a * 256 + (u + 1) * P],
+                        ident[:],
+                    )
+            wg = wstage.tile([P, 4 * O], BF16, align_bytes=64)
+            nc.scalar.copy(
+                out=wg[:].bitcast(F32).rearrange("p (o u) -> p o u", u=2),
+                in_=wt[:].rearrange("p u o -> p o u"),
+            )
+            nc.vector.quantize_mx(
+                out=wc[:, l * O : (l + 1) * O].bitcast(FP8X4),
+                scales=ws[:, l * O : (l + 1) * O],
+                in_=wg[:],
+            )
+
+        def front(c):
+            xt = ps_x.tile([P, TPC, 2, P], F32)
+            for tl in range(TPC):
+                t = c * TPC + tl
+                for u in range(2):
+                    nc.tensor.transpose(
+                        xt[:, tl, u, :], x_w[:, t * 256 + u * P : t * 256 + (u + 1) * P], ident[:]
+                    )
+            xg = xgp.tile([P, CW], BF16, align_bytes=64)
+            nc.scalar.copy(
+                out=xg[:].bitcast(F32).rearrange("p (t m u) -> p t m u", t=TPC, u=2),
+                in_=xt[:].rearrange("p t u m -> p t m u"),
+            )
+            wa = f32p.tile([P, CW], F32)
+            wb = f32p.tile([P, CW], F32)
+            q0 = f32p.tile([P, CW], F32)
+            q1 = f32p.tile([P, CW], F32)
+            nc.scalar.activation(out=wa[:], in_=xg[:], func=ACT.Abs, scale=2.5, bias=0.5)
+            nc.scalar.activation(out=wb[:], in_=xg[:], func=ACT.Abs, scale=2.5, bias=1.5)
+            nc.scalar.activation(out=wa[:], in_=wa[:], func=ACT.Abs, scale=-1.0, bias=2.0)
+            nc.scalar.activation(out=wb[:], in_=wb[:], func=ACT.Abs, scale=-1.0, bias=2.0)
+            nc.scalar.activation(out=q0[:], in_=wa[:], func=ACT.Square, scale=RS3, bias=-RS3)
+            nc.scalar.activation(out=q1[:], in_=wb[:], func=ACT.Square, scale=RS3, bias=-RS3)
+            nc.vector.scalar_tensor_tensor(out=q0[:], in0=wa[:], scalar=-1.0, in1=q0[:], op0=ALU.add, op1=ALU.mult)
+            nc.vector.scalar_tensor_tensor(out=q1[:], in0=wb[:], scalar=-1.0, in1=q1[:], op0=ALU.add, op1=ALU.mult)
+            nc.vector.scalar_tensor_tensor(out=wa[:], in0=wa[:], scalar=-1.0, in1=q0[:], op0=ALU.add, op1=ALU.subtract)
+            nc.vector.scalar_tensor_tensor(out=wb[:], in0=wb[:], scalar=-1.0, in1=q1[:], op0=ALU.add, op1=ALU.subtract)
+            nc.scalar.activation(out=q0[:], in_=q0[:], func=ACT.Abs, scale=0.5)
+            nc.scalar.activation(out=q1[:], in_=q1[:], func=ACT.Abs, scale=0.5)
+
+            sg = b16p.tile([P, 4 * CW], BF16)
+            for t in range(4):
+                nc.vector.tensor_scalar(
+                    out=sg[:, t * CW : (t + 1) * CW], in0=xg[:], scalar1=KNOT[t], scalar2=0.5,
+                    op0=(ALU.is_ge if t < 2 else ALU.is_lt), op1=ALU.subtract,
+                )
+            vt = b16p.tile([P, 4 * CW], BF16)
+            nc.vector.scalar_tensor_tensor(out=vt[:, 0:CW], in0=wb[:], scalar=0.0, in1=q0[:], op0=ALU.min, op1=ALU.subtract)
+            nc.vector.scalar_tensor_tensor(out=vt[:, CW : 2 * CW], in0=wa[:], scalar=0.0, in1=q1[:], op0=ALU.min, op1=ALU.subtract)
+            nc.vector.scalar_tensor_tensor(out=vt[:, 2 * CW : 3 * CW], in0=wb[:], scalar=0.0, in1=q0[:], op0=ALU.max, op1=ALU.add)
+            nc.vector.scalar_tensor_tensor(out=vt[:, 3 * CW : 4 * CW], in0=wa[:], scalar=0.0, in1=q1[:], op0=ALU.max, op1=ALU.add)
+            nc.vector.tensor_tensor(out=vt[:], in0=vt[:], in1=sg[:], op=ALU.mult)
+            npos = b16p.tile([P, 4 * CW], BF16, align_bytes=64)
+            nneg = b16p.tile([P, 4 * CW], BF16, align_bytes=64)
+            nc.vector.tensor_scalar(out=npos[:], in0=vt[:], scalar1=2.0, scalar2=0.0, op0=ALU.mult, op1=ALU.max)
+            nc.scalar.activation(out=nneg[:], in_=vt[:], func=ACT.Relu, scale=-2.0)
+
+            bc = codep.tile([P, 9 * WW], U32, align_bytes=64)
+            bs = codep.tile([P, 9 * WW], U8, align_bytes=64)
+            nc.vector.quantize_mx(out=bc[:, 8 * WW : 9 * WW].bitcast(FP8X4), scales=bs[:, 8 * WW : 9 * WW], in_=xg[:])
+            nc.vector.quantize_mx(out=bc[:, 0 : 4 * WW].bitcast(FP8X4), scales=bs[:, 0 : 4 * WW], in_=npos[:])
+            nc.vector.quantize_mx(out=bc[:, 4 * WW : 8 * WW].bitcast(FP8X4), scales=bs[:, 4 * WW : 8 * WW], in_=nneg[:])
+            return bc, bs
+
+        def back(c, bc, bs):
+            acc = ps_o.tile([P, TPC, O], F32)
+            for tl in range(TPC):
+                for l in range(9):
+                    lo = l * WW + tl * P
+                    nc.tensor.matmul_mx(
+                        out=acc[:, tl, :],
+                        lhsT=bc[:, lo : lo + P].bitcast(FP8X4),
+                        lhsT_scale=bs[:, lo : lo + P],
+                        rhs=wc[:, l * O : (l + 1) * O].bitcast(FP8X4),
+                        rhs_scale=ws[:, l * O : (l + 1) * O],
+                        start=(l == 0),
+                        stop=(l == 8),
+                    )
+            osb = outp.tile([P, TPC, O], F32)
+            nc.scalar.copy(out=osb[:], in_=acc[:])
+            nc.sync.dma_start(out=out_v[:, c * TPC : (c + 1) * TPC, :], in_=osb[:])
+
+        for c in range(NCH):
+            bc, bs = front(c)
+            if c == 0:
+                for l in range(9):
+                    weights_pass(l)
+            back(c, bc, bs)

@@ -30,19 +30,21 @@ def tile_kanlayer_t_kernel(tc, x, base_weight, spline_weight, out):
     nc = tc.nc
     with ExitStack() as ctx:
         const = ctx.enter_context(tc.tile_pool(name="const", bufs=1))
-        wstage = ctx.enter_context(tc.tile_pool(name="wstage", bufs=2))
+        wrp = ctx.enter_context(tc.tile_pool(name="wrp", bufs=4))
+        wgp = ctx.enter_context(tc.tile_pool(name="wgp", bufs=5))
         xgp = ctx.enter_context(tc.tile_pool(name="xgp", bufs=3))
         f32p = ctx.enter_context(tc.tile_pool(name="f32p", bufs=2))
+        sgp = ctx.enter_context(tc.tile_pool(name="sgp", bufs=1))
         b16p = ctx.enter_context(tc.tile_pool(name="b16p", bufs=2))
-        codep = ctx.enter_context(tc.tile_pool(name="codep", bufs=2))
+        codep = ctx.enter_context(tc.tile_pool(name="codep", bufs=3))
         outp = ctx.enter_context(tc.tile_pool(name="outp", bufs=3))
         ps_x = ctx.enter_context(tc.psum_pool(name="ps_x", bufs=2))
-        ps_w = ctx.enter_context(tc.psum_pool(name="ps_w", bufs=2))
+        ps_w = ctx.enter_context(tc.psum_pool(name="ps_w", bufs=4))
         ps_o = ctx.enter_context(tc.psum_pool(name="ps_o", bufs=2))
+        ctx.enter_context(tc.manual_schedule())
 
         ident = const.tile([P, P], F32)
         make_identity(nc, ident[:])
-
         x_sb = const.tile([P, NT * I], BF16)
         sw_sb = const.tile([P, 2 * I * L], BF16)
         bw_sb = const.tile([P, 2 * I], BF16)
@@ -69,18 +71,20 @@ def tile_kanlayer_t_kernel(tc, x, base_weight, spline_weight, out):
             load_x(j)
 
         x_w = x_sb[:].bitcast(F32)
+        st = {}
 
-        def weights_pass(l):
-            if l < L:
-                wr = wstage.tile([P, 2 * I], BF16)
-                nc.scalar.copy(
-                    out=wr[:].rearrange("p (a i) -> p a i", a=2),
-                    in_=sw_sb[:].rearrange("p (a i l) -> p l a i", a=2, l=L)[:, l],
-                )
-                src = wr
+        def w_reorder(l, eng):
+            wr = wrp.tile([P, 2 * I], BF16)
+            dst = wr[:].rearrange("p (a i) -> p a i", a=2)
+            src = sw_sb[:].rearrange("p (a i l) -> p l a i", a=2, l=L)[:, l]
+            if eng == "v":
+                nc.vector.tensor_copy(out=dst, in_=src)
             else:
-                src = bw_sb
-            src_w = src[:].bitcast(F32)
+                nc.scalar.copy(out=dst, in_=src)
+            st[("wr", l)] = wr
+
+        def w_transpose(l):
+            src_w = (st[("wr", l)] if l < L else bw_sb)[:].bitcast(F32)
             wt = ps_w.tile([P, 2, O], F32)
             for a in range(2):
                 for u in range(2):
@@ -89,18 +93,24 @@ def tile_kanlayer_t_kernel(tc, x, base_weight, spline_weight, out):
                         src_w[:, a * 256 + u * P : a * 256 + (u + 1) * P],
                         ident[:],
                     )
-            wg = wstage.tile([P, 4 * O], BF16, align_bytes=64)
+            st[("wt", l)] = wt
+
+        def w_evac(l):
+            wg = wgp.tile([P, 4 * O], BF16, align_bytes=64)
             nc.scalar.copy(
                 out=wg[:].bitcast(F32).rearrange("p (o u) -> p o u", u=2),
-                in_=wt[:].rearrange("p u o -> p o u"),
+                in_=st[("wt", l)][:].rearrange("p u o -> p o u"),
             )
+            st[("wg", l)] = wg
+
+        def w_quant(l):
             nc.vector.quantize_mx(
                 out=wc[:, l * O : (l + 1) * O].bitcast(FP8X4),
                 scales=ws[:, l * O : (l + 1) * O],
-                in_=wg[:],
+                in_=st[("wg", l)][:],
             )
 
-        def front(c):
+        def t_x(c):
             xt = ps_x.tile([P, TPC, 2, P], F32)
             for tl in range(TPC):
                 t = c * TPC + tl
@@ -108,10 +118,13 @@ def tile_kanlayer_t_kernel(tc, x, base_weight, spline_weight, out):
                     nc.tensor.transpose(
                         xt[:, tl, u, :], x_w[:, t * 256 + u * P : t * 256 + (u + 1) * P], ident[:]
                     )
+            st[("xt", c)] = xt
+
+        def s_front(c):
             xg = xgp.tile([P, CW], BF16, align_bytes=64)
             nc.scalar.copy(
                 out=xg[:].bitcast(F32).rearrange("p (t m u) -> p t m u", t=TPC, u=2),
-                in_=xt[:].rearrange("p t u m -> p t m u"),
+                in_=st[("xt", c)][:].rearrange("p t u m -> p t m u"),
             )
             wa = f32p.tile([P, CW], F32)
             wb = f32p.tile([P, CW], F32)
@@ -123,38 +136,70 @@ def tile_kanlayer_t_kernel(tc, x, base_weight, spline_weight, out):
             nc.scalar.activation(out=wb[:], in_=wb[:], func=ACT.Abs, scale=-1.0, bias=2.0)
             nc.scalar.activation(out=q0[:], in_=wa[:], func=ACT.Square, scale=RS3, bias=-RS3)
             nc.scalar.activation(out=q1[:], in_=wb[:], func=ACT.Square, scale=RS3, bias=-RS3)
+            st[("xg", c)] = xg
+            st[("f", c)] = (wa, wb, q0, q1)
+
+        def v_ck(c):
+            wa, wb, q0, q1 = st[("f", c)]
             nc.vector.scalar_tensor_tensor(out=q0[:], in0=wa[:], scalar=-1.0, in1=q0[:], op0=ALU.add, op1=ALU.mult)
             nc.vector.scalar_tensor_tensor(out=q1[:], in0=wb[:], scalar=-1.0, in1=q1[:], op0=ALU.add, op1=ALU.mult)
             nc.vector.scalar_tensor_tensor(out=wa[:], in0=wa[:], scalar=-1.0, in1=q0[:], op0=ALU.add, op1=ALU.subtract)
             nc.vector.scalar_tensor_tensor(out=wb[:], in0=wb[:], scalar=-1.0, in1=q1[:], op0=ALU.add, op1=ALU.subtract)
+
+        def s_abs(c):
+            wa, wb, q0, q1 = st[("f", c)]
             nc.scalar.activation(out=q0[:], in_=q0[:], func=ACT.Abs, scale=0.5)
             nc.scalar.activation(out=q1[:], in_=q1[:], func=ACT.Abs, scale=0.5)
 
-            sg = b16p.tile([P, 4 * CW], BF16)
+        def v_masks(c):
+            xg = st[("xg", c)]
+            sg = sgp.tile([P, 4 * CW], BF16)
             for t in range(4):
                 nc.vector.tensor_scalar(
                     out=sg[:, t * CW : (t + 1) * CW], in0=xg[:], scalar1=KNOT[t], scalar2=0.5,
                     op0=(ALU.is_ge if t < 2 else ALU.is_lt), op1=ALU.subtract,
                 )
+            st[("sg", c)] = sg
+
+        def v_stage2(c):
+            wa, wb, q0, q1 = st[("f", c)]
             vt = b16p.tile([P, 4 * CW], BF16)
             nc.vector.scalar_tensor_tensor(out=vt[:, 0:CW], in0=wb[:], scalar=0.0, in1=q0[:], op0=ALU.min, op1=ALU.subtract)
             nc.vector.scalar_tensor_tensor(out=vt[:, CW : 2 * CW], in0=wa[:], scalar=0.0, in1=q1[:], op0=ALU.min, op1=ALU.subtract)
             nc.vector.scalar_tensor_tensor(out=vt[:, 2 * CW : 3 * CW], in0=wb[:], scalar=0.0, in1=q0[:], op0=ALU.max, op1=ALU.add)
             nc.vector.scalar_tensor_tensor(out=vt[:, 3 * CW : 4 * CW], in0=wa[:], scalar=0.0, in1=q1[:], op0=ALU.max, op1=ALU.add)
-            nc.vector.tensor_tensor(out=vt[:], in0=vt[:], in1=sg[:], op=ALU.mult)
-            npos = b16p.tile([P, 4 * CW], BF16, align_bytes=64)
-            nneg = b16p.tile([P, 4 * CW], BF16, align_bytes=64)
-            nc.vector.tensor_scalar(out=npos[:], in0=vt[:], scalar1=2.0, scalar2=0.0, op0=ALU.mult, op1=ALU.max)
-            nc.scalar.activation(out=nneg[:], in_=vt[:], func=ACT.Relu, scale=-2.0)
+            st[("vt", c)] = vt
 
+        def v_qx(c):
             bc = codep.tile([P, 9 * WW], U32, align_bytes=64)
             bs = codep.tile([P, 9 * WW], U8, align_bytes=64)
-            nc.vector.quantize_mx(out=bc[:, 8 * WW : 9 * WW].bitcast(FP8X4), scales=bs[:, 8 * WW : 9 * WW], in_=xg[:])
-            nc.vector.quantize_mx(out=bc[:, 0 : 4 * WW].bitcast(FP8X4), scales=bs[:, 0 : 4 * WW], in_=npos[:])
-            nc.vector.quantize_mx(out=bc[:, 4 * WW : 8 * WW].bitcast(FP8X4), scales=bs[:, 4 * WW : 8 * WW], in_=nneg[:])
-            return bc, bs
+            nc.vector.quantize_mx(out=bc[:, 8 * WW : 9 * WW].bitcast(FP8X4), scales=bs[:, 8 * WW : 9 * WW], in_=st[("xg", c)][:])
+            st[("b", c)] = (bc, bs)
 
-        def back(c, bc, bs):
+        def v_mult(c):
+            vt = st[("vt", c)]
+            nc.vector.tensor_tensor(out=vt[:], in0=vt[:], in1=st[("sg", c)][:], op=ALU.mult)
+
+        def v_npos(c):
+            npos = b16p.tile([P, 4 * CW], BF16, align_bytes=64)
+            nc.vector.tensor_scalar(out=npos[:], in0=st[("vt", c)][:], scalar1=2.0, scalar2=0.0, op0=ALU.mult, op1=ALU.max)
+            st[("np", c)] = npos
+
+        def nneg_step(c, eng):
+            nneg = b16p.tile([P, 4 * CW], BF16, align_bytes=64)
+            if eng == "v":
+                nc.vector.tensor_scalar(out=nneg[:], in0=st[("vt", c)][:], scalar1=-2.0, scalar2=0.0, op0=ALU.mult, op1=ALU.max)
+            else:
+                nc.scalar.activation(out=nneg[:], in_=st[("vt", c)][:], func=ACT.Relu, scale=-2.0)
+            st[("nn", c)] = nneg
+
+        def v_qpn(c):
+            bc, bs = st[("b", c)]
+            nc.vector.quantize_mx(out=bc[:, 0 : 4 * WW].bitcast(FP8X4), scales=bs[:, 0 : 4 * WW], in_=st[("np", c)][:])
+            nc.vector.quantize_mx(out=bc[:, 4 * WW : 8 * WW].bitcast(FP8X4), scales=bs[:, 4 * WW : 8 * WW], in_=st[("nn", c)][:])
+
+        def mm(c):
+            bc, bs = st[("b", c)]
             acc = ps_o.tile([P, TPC, O], F32)
             for tl in range(TPC):
                 for l in range(9):
@@ -168,13 +213,72 @@ def tile_kanlayer_t_kernel(tc, x, base_weight, spline_weight, out):
                         start=(l == 0),
                         stop=(l == 8),
                     )
+            st[("acc", c)] = acc
+
+        def evac_out(c):
             osb = outp.tile([P, TPC, O], F32)
-            nc.scalar.copy(out=osb[:], in_=acc[:])
+            nc.scalar.copy(out=osb[:], in_=st[("acc", c)][:])
             nc.sync.dma_start(out=out_v[:, c * TPC : (c + 1) * TPC, :], in_=osb[:])
 
-        for c in range(NCH):
-            bc, bs = front(c)
-            if c == 0:
-                for l in range(9):
-                    weights_pass(l)
-            back(c, bc, bs)
+        t_x(0)
+        s_front(0)
+        for l in range(4):
+            w_reorder(l, "v")
+        t_x(1)
+        for l in range(4):
+            w_transpose(l)
+        v_masks(0)
+
+        last = NCH - 1
+        for i in range(NCH):
+            v_ck(i)
+            if i == 0:
+                w_reorder(4, "s")
+                w_reorder(5, "s")
+            if i >= 1:
+                nneg_step(i - 1, "s")
+            s_abs(i)
+            if i >= 1:
+                v_qpn(i - 1)
+            if i == 1:
+                for l in range(4):
+                    w_quant(l)
+            if i >= 1 and i + 1 < NCH:
+                t_x(i + 1)
+            if i == 1:
+                for l in range(4, 8):
+                    w_transpose(l)
+            if i == 2:
+                for l in range(4, 9):
+                    w_quant(l)
+            if i >= 2:
+                mm(i - 2)
+            if i >= 3:
+                evac_out(i - 3)
+            if i + 1 < NCH:
+                s_front(i + 1)
+            if i == 0:
+                w_reorder(6, "s")
+                w_reorder(7, "s")
+                for l in range(4):
+                    w_evac(l)
+            if i == 1:
+                w_evac(4)
+                w_transpose(8)
+                for l in range(5, 9):
+                    w_evac(l)
+            v_stage2(i)
+            v_qx(i)
+            v_mult(i)
+            if i + 1 < NCH:
+                v_masks(i + 1)
+            v_npos(i)
+            if i == last:
+                nneg_step(i, "v")
+
+        mm(last - 1)
+        evac_out(last - 2)
+        v_qpn(last)
+        mm(last)
+        evac_out(last - 1)
+        evac_out(last)

@@ -59,11 +59,11 @@ def tile_kanlayer_t_kernel(tc, x, base_weight, spline_weight, out):
             nc.sync.dma_start(out=x_t[:, 4 * j : 4 * j + 4, :], in_=x_v[:, 4 * j : 4 * j + 4, :])
 
         load_x(0)
-        nc.sync.dma_start(
+        nc.scalar.dma_start(
             out=sw_sb[:].rearrange("p (a k) -> p a k", a=2),
             in_=spline_weight.rearrange("(a p) i l -> p a (i l)", p=P),
         )
-        nc.sync.dma_start(
+        nc.scalar.dma_start(
             out=bw_sb[:].rearrange("p (a k) -> p a k", a=2),
             in_=base_weight.rearrange("(a p) i -> p a i", p=P),
         )
@@ -278,7 +278,37 @@ def tile_kanlayer_t_kernel(tc, x, base_weight, spline_weight, out):
 
         mm(last - 1)
         evac_out(last - 2)
-        v_qpn(last)
-        mm(last)
+        bc, bs = st[("b", last)]
+        acc0 = ps_o.tile([P, TPC, O], F32, tag="acc")
+        acc1 = ps_w.tile([P, 2, O], F32, tag="wt")
+        dsts = [acc0[:, 0, :], acc1[:, 0, :]]
+
+        def end_passes(ls):
+            for l in ls:
+                for tl in range(TPC):
+                    lo = l * WW + tl * P
+                    nc.tensor.matmul_mx(
+                        out=dsts[tl],
+                        lhsT=bc[:, lo : lo + P].bitcast(FP8X4),
+                        lhsT_scale=bs[:, lo : lo + P],
+                        rhs=wc[:, l * O : (l + 1) * O].bitcast(FP8X4),
+                        rhs_scale=ws[:, l * O : (l + 1) * O],
+                        start=(l == 8),
+                        stop=(l == 7),
+                    )
+
+        nc.vector.quantize_mx(out=bc[:, 0 : 4 * WW].bitcast(FP8X4), scales=bs[:, 0 : 4 * WW], in_=st[("np", last)][:])
+        end_passes([8, 0, 1, 2, 3])
         evac_out(last - 1)
-        evac_out(last)
+        nn = st[("nn", last)]
+        for h in range(2):
+            nc.vector.quantize_mx(
+                out=bc[:, (4 + 2 * h) * WW : (6 + 2 * h) * WW].bitcast(FP8X4),
+                scales=bs[:, (4 + 2 * h) * WW : (6 + 2 * h) * WW],
+                in_=nn[:, 2 * h * CW : (2 * h + 2) * CW],
+            )
+            end_passes([4 + 2 * h, 5 + 2 * h])
+        osb = outp.tile([P, TPC, O], F32, tag="osb")
+        nc.scalar.copy(out=osb[:, 0, :], in_=dsts[0])
+        nc.vector.tensor_copy(out=osb[:, 1, :], in_=dsts[1])
+        nc.sync.dma_start(out=out_v[:, last * TPC : (last + 1) * TPC, :], in_=osb[:])

@@ -59,11 +59,11 @@ def tile_kanlayer_t_kernel(tc, x, base_weight, spline_weight, out):
             nc.sync.dma_start(out=x_t[:, 4 * j : 4 * j + 4, :], in_=x_v[:, 4 * j : 4 * j + 4, :])
 
         load_x(0)
-        nc.scalar.dma_start(
+        nc.sync.dma_start(
             out=sw_sb[:].rearrange("p (a k) -> p a k", a=2),
             in_=spline_weight.rearrange("(a p) i l -> p a (i l)", p=P),
         )
-        nc.scalar.dma_start(
+        nc.sync.dma_start(
             out=bw_sb[:].rearrange("p (a k) -> p a k", a=2),
             in_=base_weight.rearrange("(a p) i -> p a i", p=P),
         )
@@ -182,7 +182,8 @@ def tile_kanlayer_t_kernel(tc, x, base_weight, spline_weight, out):
 
         def v_npos(c):
             npos = b16p.tile([P, 4 * CW], BF16, align_bytes=64)
-            nc.vector.tensor_scalar(out=npos[:], in0=st[("vt", c)][:], scalar1=2.0, scalar2=0.0, op0=ALU.mult, op1=ALU.max)
+            vw = 4 * CW if c == NCH - 1 else 3 * CW
+            nc.vector.tensor_scalar(out=npos[:, 0:vw], in0=st[("vt", c)][:, 0:vw], scalar1=2.0, scalar2=0.0, op0=ALU.mult, op1=ALU.max)
             st[("np", c)] = npos
 
         def nneg_step(c, eng):
@@ -190,6 +191,7 @@ def tile_kanlayer_t_kernel(tc, x, base_weight, spline_weight, out):
             if eng == "v":
                 nc.vector.tensor_scalar(out=nneg[:], in0=st[("vt", c)][:], scalar1=-2.0, scalar2=0.0, op0=ALU.mult, op1=ALU.max)
             else:
+                nc.scalar.activation(out=st[("np", c)][:, 3 * CW : 4 * CW], in_=st[("vt", c)][:, 3 * CW : 4 * CW], func=ACT.Relu, scale=2.0)
                 nc.scalar.activation(out=nneg[:], in_=st[("vt", c)][:], func=ACT.Relu, scale=-2.0)
             st[("nn", c)] = nneg
 
@@ -278,37 +280,7 @@ def tile_kanlayer_t_kernel(tc, x, base_weight, spline_weight, out):
 
         mm(last - 1)
         evac_out(last - 2)
-        bc, bs = st[("b", last)]
-        acc0 = ps_o.tile([P, TPC, O], F32, tag="acc")
-        acc1 = ps_w.tile([P, 2, O], F32, tag="wt")
-        dsts = [acc0[:, 0, :], acc1[:, 0, :]]
-
-        def end_passes(ls):
-            for l in ls:
-                for tl in range(TPC):
-                    lo = l * WW + tl * P
-                    nc.tensor.matmul_mx(
-                        out=dsts[tl],
-                        lhsT=bc[:, lo : lo + P].bitcast(FP8X4),
-                        lhsT_scale=bs[:, lo : lo + P],
-                        rhs=wc[:, l * O : (l + 1) * O].bitcast(FP8X4),
-                        rhs_scale=ws[:, l * O : (l + 1) * O],
-                        start=(l == 8),
-                        stop=(l == 7),
-                    )
-
-        nc.vector.quantize_mx(out=bc[:, 0 : 4 * WW].bitcast(FP8X4), scales=bs[:, 0 : 4 * WW], in_=st[("np", last)][:])
-        end_passes([8, 0, 1, 2, 3])
+        v_qpn(last)
+        mm(last)
         evac_out(last - 1)
-        nn = st[("nn", last)]
-        for h in range(2):
-            nc.vector.quantize_mx(
-                out=bc[:, (4 + 2 * h) * WW : (6 + 2 * h) * WW].bitcast(FP8X4),
-                scales=bs[:, (4 + 2 * h) * WW : (6 + 2 * h) * WW],
-                in_=nn[:, 2 * h * CW : (2 * h + 2) * CW],
-            )
-            end_passes([4 + 2 * h, 5 + 2 * h])
-        osb = outp.tile([P, TPC, O], F32, tag="osb")
-        nc.scalar.copy(out=osb[:, 0, :], in_=dsts[0])
-        nc.vector.tensor_copy(out=osb[:, 1, :], in_=dsts[1])
-        nc.sync.dma_start(out=out_v[:, last * TPC : (last + 1) * TPC, :], in_=osb[:])
+        evac_out(last)

@@ -22,8 +22,20 @@ NCH = NT // TPC
 CW = TPC * P * 4
 WW = CW // 4
 FLOPS = 2 * B * O * (I + I * L)
-RS3 = 1.0 / math.sqrt(3.0)
-KNOT = [-2.2 + 0.4 * (t + 4) for t in range(4)]
+R6 = 1.0 / math.sqrt(6.0)
+STEEP = 1024.0
+NV = 11
+AN, BN, DN, CN, W2, W1, S6, S1, S0, S7, XB = range(NV)
+NW = 13
+NEG = {2: 9, 4: 10, 3: 11, 5: 12}
+BASE = 8
+PASSES = [
+    (XB, BASE),
+    (AN, NEG[4]), (DN, NEG[4]), (BN, NEG[3]), (CN, NEG[3]),
+    (W2, 4), (W2, NEG[2]), (W1, 3), (W1, NEG[5]),
+    (S6, 6), (S6, NEG[2]), (S1, 1), (S1, NEG[5]),
+    (S0, 0), (S0, 4), (S7, 7), (S7, 3),
+]
 
 
 def tile_kanlayer_t_kernel(tc, x, base_weight, spline_weight, out):
@@ -32,12 +44,14 @@ def tile_kanlayer_t_kernel(tc, x, base_weight, spline_weight, out):
         const = ctx.enter_context(tc.tile_pool(name="const", bufs=1))
         wrp = ctx.enter_context(tc.tile_pool(name="wrp", bufs=4))
         wgp = ctx.enter_context(tc.tile_pool(name="wgp", bufs=5))
+        wnp = ctx.enter_context(tc.tile_pool(name="wnp", bufs=2))
         xgp = ctx.enter_context(tc.tile_pool(name="xgp", bufs=3))
         f32p = ctx.enter_context(tc.tile_pool(name="f32p", bufs=2))
-        sgp = ctx.enter_context(tc.tile_pool(name="sgp", bufs=1))
+        mp = ctx.enter_context(tc.tile_pool(name="mp", bufs=3))
+        one = ctx.enter_context(tc.tile_pool(name="one", bufs=1))
         b16p = ctx.enter_context(tc.tile_pool(name="b16p", bufs=2))
         codep = ctx.enter_context(tc.tile_pool(name="codep", bufs=3))
-        outp = ctx.enter_context(tc.tile_pool(name="outp", bufs=3))
+        outp = ctx.enter_context(tc.tile_pool(name="outp", bufs=2))
         ps_x = ctx.enter_context(tc.psum_pool(name="ps_x", bufs=2))
         ps_w = ctx.enter_context(tc.psum_pool(name="ps_w", bufs=4))
         ps_o = ctx.enter_context(tc.psum_pool(name="ps_o", bufs=2))
@@ -48,8 +62,8 @@ def tile_kanlayer_t_kernel(tc, x, base_weight, spline_weight, out):
         x_sb = const.tile([P, NT * I], BF16)
         sw_sb = const.tile([P, 2 * I * L], BF16)
         bw_sb = const.tile([P, 2 * I], BF16)
-        wc = const.tile([P, 9 * O], U32, align_bytes=64)
-        ws = const.tile([P, 9 * O], U8, align_bytes=64)
+        wc = const.tile([P, NW * O], U32, align_bytes=64)
+        ws = const.tile([P, NW * O], U8, align_bytes=64)
 
         x_v = x.rearrange("(p t) i -> p t i", t=NT)
         x_t = x_sb[:].rearrange("p (t i) -> p t i", i=I)
@@ -73,14 +87,12 @@ def tile_kanlayer_t_kernel(tc, x, base_weight, spline_weight, out):
         x_w = x_sb[:].bitcast(F32)
         st = {}
 
-        def w_reorder(l, eng):
+        def w_reorder(l):
             wr = wrp.tile([P, 2 * I], BF16)
-            dst = wr[:].rearrange("p (a i) -> p a i", a=2)
-            src = sw_sb[:].rearrange("p (a i l) -> p l a i", a=2, l=L)[:, l]
-            if eng == "v":
-                nc.vector.tensor_copy(out=dst, in_=src)
-            else:
-                nc.scalar.copy(out=dst, in_=src)
+            nc.vector.tensor_copy(
+                out=wr[:].rearrange("p (a i) -> p a i", a=2),
+                in_=sw_sb[:].rearrange("p (a i l) -> p l a i", a=2, l=L)[:, l],
+            )
             st[("wr", l)] = wr
 
         def w_transpose(l):
@@ -103,12 +115,18 @@ def tile_kanlayer_t_kernel(tc, x, base_weight, spline_weight, out):
             )
             st[("wg", l)] = wg
 
-        def w_quant(l):
+        def w_quant_into(n, wg):
             nc.vector.quantize_mx(
-                out=wc[:, l * O : (l + 1) * O].bitcast(FP8X4),
-                scales=ws[:, l * O : (l + 1) * O],
-                in_=st[("wg", l)][:],
+                out=wc[:, n * O : (n + 1) * O].bitcast(FP8X4), scales=ws[:, n * O : (n + 1) * O], in_=wg[:]
             )
+
+        def w_quant(l):
+            wg = st[("wg", l)]
+            w_quant_into(l, wg)
+            if l in NEG:
+                wn = wnp.tile([P, 4 * O], BF16, align_bytes=64)
+                nc.vector.tensor_scalar(out=wn[:], in0=wg[:], scalar1=-1.0, scalar2=None, op0=ALU.mult)
+                w_quant_into(NEG[l], wn)
 
         def t_x(c):
             xt = ps_x.tile([P, TPC, 2, P], F32)
@@ -120,100 +138,102 @@ def tile_kanlayer_t_kernel(tc, x, base_weight, spline_weight, out):
                     )
             st[("xt", c)] = xt
 
-        def s_front(c):
+        def s_copy(c):
             xg = xgp.tile([P, CW], BF16, align_bytes=64)
             nc.scalar.copy(
                 out=xg[:].bitcast(F32).rearrange("p (t m u) -> p t m u", t=TPC, u=2),
                 in_=st[("xt", c)][:].rearrange("p t u m -> p t m u"),
             )
-            wa = f32p.tile([P, CW], F32)
-            wb = f32p.tile([P, CW], F32)
-            q0 = f32p.tile([P, CW], F32)
-            q1 = f32p.tile([P, CW], F32)
-            nc.scalar.activation(out=wa[:], in_=xg[:], func=ACT.Abs, scale=2.5, bias=0.5)
-            nc.scalar.activation(out=wb[:], in_=xg[:], func=ACT.Abs, scale=2.5, bias=1.5)
-            nc.scalar.activation(out=wa[:], in_=wa[:], func=ACT.Abs, scale=-1.0, bias=2.0)
-            nc.scalar.activation(out=wb[:], in_=wb[:], func=ACT.Abs, scale=-1.0, bias=2.0)
-            nc.scalar.activation(out=q0[:], in_=wa[:], func=ACT.Square, scale=RS3, bias=-RS3)
-            nc.scalar.activation(out=q1[:], in_=wb[:], func=ACT.Square, scale=RS3, bias=-RS3)
             st[("xg", c)] = xg
-            st[("f", c)] = (wa, wb, q0, q1)
 
-        def v_ck(c):
-            wa, wb, q0, q1 = st[("f", c)]
-            nc.vector.scalar_tensor_tensor(out=q0[:], in0=wa[:], scalar=-1.0, in1=q0[:], op0=ALU.add, op1=ALU.mult)
-            nc.vector.scalar_tensor_tensor(out=q1[:], in0=wb[:], scalar=-1.0, in1=q1[:], op0=ALU.add, op1=ALU.mult)
-            nc.vector.scalar_tensor_tensor(out=wa[:], in0=wa[:], scalar=-1.0, in1=q0[:], op0=ALU.add, op1=ALU.subtract)
-            nc.vector.scalar_tensor_tensor(out=wb[:], in0=wb[:], scalar=-1.0, in1=q1[:], op0=ALU.add, op1=ALU.subtract)
+        def s_front(c):
+            xg = st[("xg", c)]
+            f = f32p.tile([P, 2 * CW], F32)
+            m = mp.tile([P, 2 * CW], BF16)
+            q = f32p.tile([P, 2 * CW], F32)
+            u = f32p.tile([P, CW], F32)
+            nc.scalar.activation(out=f[:, 0:CW], in_=xg[:], func=ACT.Abs, scale=2.5, bias=-0.5)
+            nc.scalar.activation(out=f[:, CW : 2 * CW], in_=xg[:], func=ACT.Abs, scale=2.5, bias=0.5)
+            nc.scalar.activation(out=m[:], in_=f[:], func=ACT.Identity, scale=-STEEP, bias=STEEP - 1.0 / 6.0)
+            nc.scalar.activation(out=f[:], in_=f[:], func=ACT.Abs, scale=-1.0, bias=1.0)
+            nc.scalar.activation(out=q[:], in_=f[:], func=ACT.Square, scale=R6, bias=-R6)
+            nc.scalar.activation(out=u[:], in_=f[:, 0:CW], func=ACT.Abs, scale=-1.0, bias=1.0)
+            st[("f", c)] = (f, m, q, u)
 
-        def s_abs(c):
-            wa, wb, q0, q1 = st[("f", c)]
-            nc.scalar.activation(out=q0[:], in_=q0[:], func=ACT.Abs, scale=0.5)
-            nc.scalar.activation(out=q1[:], in_=q1[:], func=ACT.Abs, scale=0.5)
+        def v_ab(c):
+            f, m, q, u = st[("f", c)]
+            p4 = b16p.tile([P, 4 * CW], BF16, align_bytes=64)
+            nc.vector.scalar_tensor_tensor(out=p4[:, 0 : 2 * CW], in0=f[:], scalar=-1.0, in1=q[:], op0=ALU.add, op1=ALU.mult)
+            st[("p4", c)] = p4
+
+        def v_d(c):
+            f, m, q, u = st[("f", c)]
+            nc.vector.scalar_tensor_tensor(out=q[:, 0:CW], in0=u[:], scalar=-2.0, in1=q[:, 0:CW], op0=ALU.add, op1=ALU.mult)
+
+        def v_c(c):
+            f, m, q, u = st[("f", c)]
+            nc.vector.scalar_tensor_tensor(out=q[:, CW : 2 * CW], in0=u[:], scalar=1.0, in1=q[:, CW : 2 * CW], op0=ALU.add, op1=ALU.mult)
+
+        def s_daff(c):
+            q = st[("f", c)][2]
+            nc.scalar.activation(out=st[("p4", c)][:, 2 * CW : 3 * CW], in_=q[:, 0:CW], func=ACT.Identity, scale=-3.0, bias=-2.0 / 3.0)
+
+        def v_caff(c):
+            q = st[("f", c)][2]
+            nc.vector.tensor_scalar(
+                out=st[("p4", c)][:, 3 * CW : 4 * CW], in0=q[:, CW : 2 * CW], scalar1=3.0, scalar2=-2.0 / 3.0,
+                op0=ALU.mult, op1=ALU.add,
+            )
+
+        def v_s07(c):
+            s07 = b16p.tile([P, 2 * CW], BF16, align_bytes=64)
+            nc.vector.tensor_scalar(out=s07[:], in0=st[("p4", c)][:, 0 : 2 * CW], scalar1=0.0, scalar2=None, op0=ALU.max)
+            st[("s07", c)] = s07
 
         def v_masks(c):
             xg = st[("xg", c)]
-            sg = sgp.tile([P, 4 * CW], BF16)
-            for t in range(4):
-                nc.vector.tensor_scalar(
-                    out=sg[:, t * CW : (t + 1) * CW], in0=xg[:], scalar1=KNOT[t], scalar2=0.5,
-                    op0=(ALU.is_ge if t < 2 else ALU.is_lt), op1=ALU.subtract,
-                )
-            st[("sg", c)] = sg
+            mk = one.tile([P, 2 * CW], BF16)
+            nc.vector.tensor_scalar(out=mk[:, 0:CW], in0=xg[:], scalar1=0.2, scalar2=-1.0, op0=ALU.is_ge, op1=ALU.mult)
+            nc.vector.tensor_scalar(out=mk[:, CW : 2 * CW], in0=xg[:], scalar1=-0.2, scalar2=-1.0, op0=ALU.is_lt, op1=ALU.mult)
+            st[("mk", c)] = mk
 
-        def v_stage2(c):
-            wa, wb, q0, q1 = st[("f", c)]
-            vt = b16p.tile([P, 4 * CW], BF16)
-            nc.vector.scalar_tensor_tensor(out=vt[:, 0:CW], in0=wb[:], scalar=0.0, in1=q0[:], op0=ALU.min, op1=ALU.subtract)
-            nc.vector.scalar_tensor_tensor(out=vt[:, CW : 2 * CW], in0=wa[:], scalar=0.0, in1=q1[:], op0=ALU.min, op1=ALU.subtract)
-            nc.vector.scalar_tensor_tensor(out=vt[:, 2 * CW : 3 * CW], in0=wb[:], scalar=0.0, in1=q0[:], op0=ALU.max, op1=ALU.add)
-            nc.vector.scalar_tensor_tensor(out=vt[:, 3 * CW : 4 * CW], in0=wa[:], scalar=0.0, in1=q1[:], op0=ALU.max, op1=ALU.add)
-            st[("vt", c)] = vt
+        def quant(c, n0, n1, src):
+            bc, bs = st[("b", c)]
+            nc.vector.quantize_mx(out=bc[:, n0 * WW : n1 * WW].bitcast(FP8X4), scales=bs[:, n0 * WW : n1 * WW], in_=src)
 
         def v_qx(c):
-            bc = codep.tile([P, 9 * WW], U32, align_bytes=64)
-            bs = codep.tile([P, 9 * WW], U8, align_bytes=64)
-            nc.vector.quantize_mx(out=bc[:, 8 * WW : 9 * WW].bitcast(FP8X4), scales=bs[:, 8 * WW : 9 * WW], in_=st[("xg", c)][:])
+            bc = codep.tile([P, NV * WW], U32, align_bytes=64)
+            bs = codep.tile([P, NV * WW], U8, align_bytes=64)
             st[("b", c)] = (bc, bs)
+            quant(c, XB, XB + 1, st[("xg", c)][:])
+
+        def v_max(c):
+            w4 = one.tile([P, 4 * CW], BF16, align_bytes=64)
+            nc.vector.tensor_tensor(out=w4[:, 0 : 2 * CW], in0=st[("p4", c)][:, 2 * CW : 4 * CW], in1=st[("f", c)][1][:], op=ALU.max)
+            st[("w4", c)] = w4
+
+        def v_min(c):
+            w4 = st[("w4", c)]
+            nc.vector.tensor_tensor(out=w4[:, 0 : 2 * CW], in0=w4[:, 0 : 2 * CW], in1=st[("p4", c)][:, 0 : 2 * CW], op=ALU.min)
 
         def v_mult(c):
-            vt = st[("vt", c)]
-            nc.vector.tensor_tensor(out=vt[:], in0=vt[:], in1=st[("sg", c)][:], op=ALU.mult)
-
-        def v_npos(c):
-            npos = b16p.tile([P, 4 * CW], BF16, align_bytes=64)
-            vw = 4 * CW if c == NCH - 1 else 3 * CW
-            nc.vector.tensor_scalar(out=npos[:, 0:vw], in0=st[("vt", c)][:, 0:vw], scalar1=2.0, scalar2=0.0, op0=ALU.mult, op1=ALU.max)
-            st[("np", c)] = npos
-
-        def nneg_step(c, eng):
-            nneg = b16p.tile([P, 4 * CW], BF16, align_bytes=64)
-            if eng == "v":
-                nc.vector.tensor_scalar(out=nneg[:], in0=st[("vt", c)][:], scalar1=-2.0, scalar2=0.0, op0=ALU.mult, op1=ALU.max)
-            else:
-                nc.scalar.activation(out=st[("np", c)][:, 3 * CW : 4 * CW], in_=st[("vt", c)][:, 3 * CW : 4 * CW], func=ACT.Relu, scale=2.0)
-                nc.scalar.activation(out=nneg[:], in_=st[("vt", c)][:], func=ACT.Relu, scale=-2.0)
-            st[("nn", c)] = nneg
-
-        def v_qpn(c):
-            bc, bs = st[("b", c)]
-            nc.vector.quantize_mx(out=bc[:, 0 : 4 * WW].bitcast(FP8X4), scales=bs[:, 0 : 4 * WW], in_=st[("np", c)][:])
-            nc.vector.quantize_mx(out=bc[:, 4 * WW : 8 * WW].bitcast(FP8X4), scales=bs[:, 4 * WW : 8 * WW], in_=st[("nn", c)][:])
+            w4 = st[("w4", c)]
+            nc.vector.tensor_tensor(out=w4[:, 2 * CW : 4 * CW], in0=w4[:, 0 : 2 * CW], in1=st[("mk", c)][:], op=ALU.mult)
 
         def mm(c):
             bc, bs = st[("b", c)]
             acc = ps_o.tile([P, TPC, O], F32)
             for tl in range(TPC):
-                for l in range(9):
-                    lo = l * WW + tl * P
+                for n, (v, w) in enumerate(PASSES):
+                    lo = v * WW + tl * P
                     nc.tensor.matmul_mx(
                         out=acc[:, tl, :],
                         lhsT=bc[:, lo : lo + P].bitcast(FP8X4),
                         lhsT_scale=bs[:, lo : lo + P],
-                        rhs=wc[:, l * O : (l + 1) * O].bitcast(FP8X4),
-                        rhs_scale=ws[:, l * O : (l + 1) * O],
-                        start=(l == 0),
-                        stop=(l == 8),
+                        rhs=wc[:, w * O : (w + 1) * O].bitcast(FP8X4),
+                        rhs_scale=ws[:, w * O : (w + 1) * O],
+                        start=(n == 0),
+                        stop=(n == len(PASSES) - 1),
                     )
             st[("acc", c)] = acc
 
@@ -223,64 +243,64 @@ def tile_kanlayer_t_kernel(tc, x, base_weight, spline_weight, out):
             nc.sync.dma_start(out=out_v[:, c * TPC : (c + 1) * TPC, :], in_=osb[:])
 
         t_x(0)
+        s_copy(0)
         s_front(0)
-        for l in range(4):
-            w_reorder(l, "v")
         t_x(1)
+        s_copy(1)
         for l in range(4):
+            w_reorder(l)
             w_transpose(l)
-        v_masks(0)
+        for l in range(4, 8):
+            w_reorder(l)
 
-        last = NCH - 1
-        for i in range(NCH):
-            v_ck(i)
+        for i in range(NCH + 1):
+            a, b = i < NCH, i >= 1
+            if i + 2 < NCH:
+                t_x(i + 2)
             if i == 0:
-                w_reorder(4, "s")
-                w_reorder(5, "s")
-            if i >= 1:
-                nneg_step(i - 1, "s")
-            s_abs(i)
-            if i >= 1:
-                v_qpn(i - 1)
-            if i == 1:
                 for l in range(4):
-                    w_quant(l)
-            if i >= 1 and i + 1 < NCH:
-                t_x(i + 1)
-            if i == 1:
+                    w_evac(l)
+            if i + 1 < NCH:
+                if i >= 1:
+                    s_copy(i + 1)
+                s_front(i + 1)
+            if a:
+                v_ab(i)
+            if b:
+                v_max(i - 1)
+            if a:
+                v_d(i)
+            if b:
+                v_min(i - 1)
+            if a:
+                v_c(i)
+            if b:
+                v_mult(i - 1)
+            if a:
+                v_s07(i)
+                v_caff(i)
+                s_daff(i)
+            if b:
+                quant(i - 1, AN, CN + 1, st[("p4", i - 1)][:])
+            if i == 0:
                 for l in range(4, 8):
                     w_transpose(l)
-            if i == 2:
+                for l in range(4):
+                    w_quant(l)
+                for l in range(4, 8):
+                    w_evac(l)
+                w_transpose(8)
+                w_evac(8)
+            if i == 1:
                 for l in range(4, 9):
                     w_quant(l)
+            if a:
+                v_masks(i)
+                v_qx(i)
+            if b:
+                quant(i - 1, W2, S1 + 1, st[("w4", i - 1)][:])
+                quant(i - 1, S0, S7 + 1, st[("s07", i - 1)][:])
+                mm(i - 1)
             if i >= 2:
-                mm(i - 2)
-            if i >= 3:
-                evac_out(i - 3)
-            if i + 1 < NCH:
-                s_front(i + 1)
-            if i == 0:
-                w_reorder(6, "s")
-                w_reorder(7, "s")
-                for l in range(4):
-                    w_evac(l)
-            if i == 1:
-                w_evac(4)
-                w_transpose(8)
-                for l in range(5, 9):
-                    w_evac(l)
-            v_stage2(i)
-            v_qx(i)
-            v_mult(i)
-            if i + 1 < NCH:
-                v_masks(i + 1)
-            v_npos(i)
-            if i == last:
-                nneg_step(i, "v")
-
-        mm(last - 1)
-        evac_out(last - 2)
-        v_qpn(last)
-        mm(last)
-        evac_out(last - 1)
-        evac_out(last)
+                evac_out(i - 2)
+        evac_out(NCH - 1)

@@ -17,10 +17,9 @@ ACT = mybir.ActivationFunctionType
 P = 128
 B, I, O, L = 4096, 512, 256, 8
 NT = B // P
-TPC = 2
-NCH = NT // TPC
-CW = TPC * P * 4
-WW = CW // 4
+LEN = [1, 1] + [2] * 14 + [1, 1]
+NCH = len(LEN)
+T0 = [sum(LEN[:c]) for c in range(NCH)]
 FLOPS = 2 * B * O * (I + I * L)
 R6 = 1.0 / math.sqrt(6.0)
 STEEP = 1024.0
@@ -42,7 +41,6 @@ def tile_kanlayer_t_kernel(tc, x, base_weight, spline_weight, out):
     nc = tc.nc
     with ExitStack() as ctx:
         const = ctx.enter_context(tc.tile_pool(name="const", bufs=1))
-        wrp = ctx.enter_context(tc.tile_pool(name="wrp", bufs=4))
         wgp = ctx.enter_context(tc.tile_pool(name="wgp", bufs=5))
         wnp = ctx.enter_context(tc.tile_pool(name="wnp", bufs=2))
         xgp = ctx.enter_context(tc.tile_pool(name="xgp", bufs=3))
@@ -59,6 +57,8 @@ def tile_kanlayer_t_kernel(tc, x, base_weight, spline_weight, out):
 
         ident = const.tile([P, P], F32)
         make_identity(nc, ident[:])
+        identb = const.tile([P, P], BF16)
+        make_identity(nc, identb[:])
         x_sb = const.tile([P, NT * I], BF16)
         sw_sb = const.tile([P, 2 * I * L], BF16)
         bw_sb = const.tile([P, 2 * I], BF16)
@@ -69,10 +69,11 @@ def tile_kanlayer_t_kernel(tc, x, base_weight, spline_weight, out):
         x_t = x_sb[:].rearrange("p (t i) -> p t i", i=I)
         out_v = out.rearrange("(p t) o -> p t o", t=NT)
 
-        def load_x(j):
-            nc.sync.dma_start(out=x_t[:, 4 * j : 4 * j + 4, :], in_=x_v[:, 4 * j : 4 * j + 4, :])
+        def load_x(t0, t1):
+            nc.sync.dma_start(out=x_t[:, t0:t1, :], in_=x_v[:, t0:t1, :])
 
-        load_x(0)
+        load_x(0, 1)
+        load_x(1, 4)
         nc.sync.dma_start(
             out=sw_sb[:].rearrange("p (a k) -> p a k", a=2),
             in_=spline_weight.rearrange("(a p) i l -> p a (i l)", p=P),
@@ -82,37 +83,44 @@ def tile_kanlayer_t_kernel(tc, x, base_weight, spline_weight, out):
             in_=base_weight.rearrange("(a p) i -> p a i", p=P),
         )
         for j in range(1, 8):
-            load_x(j)
+            load_x(4 * j, 4 * j + 4)
 
         x_w = x_sb[:].bitcast(F32)
         st = {}
 
-        def w_reorder(l):
-            wr = wrp.tile([P, 2 * I], BF16)
-            nc.vector.tensor_copy(
-                out=wr[:].rearrange("p (a i) -> p a i", a=2),
-                in_=sw_sb[:].rearrange("p (a i l) -> p l a i", a=2, l=L)[:, l],
-            )
-            st[("wr", l)] = wr
+        sw_v = sw_sb[:].rearrange("p (a u k e l) -> p a l u e k", a=2, u=2, e=2, l=L)
 
         def w_transpose(l):
-            src_w = (st[("wr", l)] if l < L else bw_sb)[:].bitcast(F32)
-            wt = ps_w.tile([P, 2, O], F32)
-            for a in range(2):
-                for u in range(2):
-                    nc.tensor.transpose(
-                        wt[:, u, a * P : (a + 1) * P],
-                        src_w[:, a * 256 + u * P : a * 256 + (u + 1) * P],
-                        ident[:],
-                    )
+            if l < L:
+                wt = ps_w.tile([P, 4, O], BF16)
+                for a in range(2):
+                    for t in range(4):
+                        nc.tensor.transpose(wt[:, t, a * P : (a + 1) * P], sw_v[:, a, l, t // 2, t % 2], identb[:])
+            else:
+                wt = ps_w.tile([P, 2, O], F32)
+                for a in range(2):
+                    for u in range(2):
+                        nc.tensor.transpose(
+                            wt[:, u, a * P : (a + 1) * P],
+                            bw_sb[:].bitcast(F32)[:, a * 256 + u * P : a * 256 + (u + 1) * P],
+                            ident[:],
+                        )
             st[("wt", l)] = wt
 
         def w_evac(l):
             wg = wgp.tile([P, 4 * O], BF16, align_bytes=64)
-            nc.scalar.copy(
-                out=wg[:].bitcast(F32).rearrange("p (o u) -> p o u", u=2),
-                in_=st[("wt", l)][:].rearrange("p u o -> p o u"),
-            )
+            if l < L:
+                dst = wg[:].rearrange("p (o t) -> p o t", t=4)
+                src = st[("wt", l)][:].rearrange("p t o -> p o t")
+                if 3 <= l < 6:
+                    nc.vector.tensor_copy(out=dst, in_=src)
+                else:
+                    nc.scalar.copy(out=dst, in_=src)
+            else:
+                nc.scalar.copy(
+                    out=wg[:].bitcast(F32).rearrange("p (o u) -> p o u", u=2),
+                    in_=st[("wt", l)][:].rearrange("p u o -> p o u"),
+                )
             st[("wg", l)] = wg
 
         def w_quant_into(n, wg):
@@ -129,9 +137,9 @@ def tile_kanlayer_t_kernel(tc, x, base_weight, spline_weight, out):
                 w_quant_into(NEG[l], wn)
 
         def t_x(c):
-            xt = ps_x.tile([P, TPC, 2, P], F32)
-            for tl in range(TPC):
-                t = c * TPC + tl
+            xt = ps_x.tile([P, LEN[c], 2, P], F32)
+            for tl in range(LEN[c]):
+                t = T0[c] + tl
                 for u in range(2):
                     nc.tensor.transpose(
                         xt[:, tl, u, :], x_w[:, t * 256 + u * P : t * 256 + (u + 1) * P], ident[:]
@@ -139,93 +147,121 @@ def tile_kanlayer_t_kernel(tc, x, base_weight, spline_weight, out):
             st[("xt", c)] = xt
 
         def s_copy(c):
-            xg = xgp.tile([P, CW], BF16, align_bytes=64)
+            cw = 512 * LEN[c]
+            xg = xgp.tile([P, cw], BF16, align_bytes=64)
             nc.scalar.copy(
-                out=xg[:].bitcast(F32).rearrange("p (t m u) -> p t m u", t=TPC, u=2),
+                out=xg[:].bitcast(F32).rearrange("p (t m u) -> p t m u", t=LEN[c], u=2),
                 in_=st[("xt", c)][:].rearrange("p t u m -> p t m u"),
             )
             st[("xg", c)] = xg
 
-        def s_front(c):
+        def s_front1(c):
+            cw = 512 * LEN[c]
             xg = st[("xg", c)]
-            f = f32p.tile([P, 2 * CW], F32)
-            m = mp.tile([P, 2 * CW], BF16)
-            q = f32p.tile([P, 2 * CW], F32)
-            u = f32p.tile([P, CW], F32)
-            nc.scalar.activation(out=f[:, 0:CW], in_=xg[:], func=ACT.Abs, scale=2.5, bias=-0.5)
-            nc.scalar.activation(out=f[:, CW : 2 * CW], in_=xg[:], func=ACT.Abs, scale=2.5, bias=0.5)
-            nc.scalar.activation(out=m[:], in_=f[:], func=ACT.Identity, scale=-STEEP, bias=STEEP - 1.0 / 6.0)
-            nc.scalar.activation(out=f[:], in_=f[:], func=ACT.Abs, scale=-1.0, bias=1.0)
+            d = one.tile([P, 2 * cw], F32)
+            nc.scalar.activation(out=d[:, 0:cw], in_=xg[:], func=ACT.Abs, scale=2.5, bias=-0.5)
+            nc.scalar.activation(out=d[:, cw : 2 * cw], in_=xg[:], func=ACT.Abs, scale=2.5, bias=0.5)
+            st[("d", c)] = d
+
+        def s_front2(c):
+            cw = 512 * LEN[c]
+            d = st[("d", c)]
+            f = f32p.tile([P, 2 * cw], F32)
+            m = mp.tile([P, 2 * cw], BF16)
+            nc.scalar.activation(out=f[:], in_=d[:], func=ACT.Abs, scale=-1.0, bias=1.0)
+            nc.scalar.activation(out=m[:], in_=d[:], func=ACT.Identity, scale=-STEEP, bias=STEEP - 1.0 / 6.0)
+            st[("a", c)] = f
+            st[("m", c)] = m
+
+        def s_front3(c):
+            cw = 512 * LEN[c]
+            f = st[("a", c)]
+            q = f32p.tile([P, 2 * cw], F32)
+            u = f32p.tile([P, cw], F32)
             nc.scalar.activation(out=q[:], in_=f[:], func=ACT.Square, scale=R6, bias=-R6)
-            nc.scalar.activation(out=u[:], in_=f[:, 0:CW], func=ACT.Abs, scale=-1.0, bias=1.0)
-            st[("f", c)] = (f, m, q, u)
+            nc.scalar.activation(out=u[:], in_=f[:, 0:cw], func=ACT.Abs, scale=-1.0, bias=1.0)
+            st[("f", c)] = (f, st[("m", c)], q, u)
 
         def v_ab(c):
+            cw = 512 * LEN[c]
             f, m, q, u = st[("f", c)]
-            p4 = b16p.tile([P, 4 * CW], BF16, align_bytes=64)
-            nc.vector.scalar_tensor_tensor(out=p4[:, 0 : 2 * CW], in0=f[:], scalar=-1.0, in1=q[:], op0=ALU.add, op1=ALU.mult)
+            p4 = b16p.tile([P, 4 * cw], BF16, align_bytes=64)
+            nc.vector.scalar_tensor_tensor(out=p4[:, 0 : 2 * cw], in0=f[:], scalar=-1.0, in1=q[:], op0=ALU.add, op1=ALU.mult)
             st[("p4", c)] = p4
 
         def v_d(c):
+            cw = 512 * LEN[c]
             f, m, q, u = st[("f", c)]
-            nc.vector.scalar_tensor_tensor(out=q[:, 0:CW], in0=u[:], scalar=-2.0, in1=q[:, 0:CW], op0=ALU.add, op1=ALU.mult)
+            nc.vector.scalar_tensor_tensor(out=q[:, 0:cw], in0=u[:], scalar=-2.0, in1=q[:, 0:cw], op0=ALU.add, op1=ALU.mult)
 
         def v_c(c):
+            cw = 512 * LEN[c]
             f, m, q, u = st[("f", c)]
-            nc.vector.scalar_tensor_tensor(out=q[:, CW : 2 * CW], in0=u[:], scalar=1.0, in1=q[:, CW : 2 * CW], op0=ALU.add, op1=ALU.mult)
+            nc.vector.scalar_tensor_tensor(out=q[:, cw : 2 * cw], in0=u[:], scalar=1.0, in1=q[:, cw : 2 * cw], op0=ALU.add, op1=ALU.mult)
 
         def s_daff(c):
+            cw = 512 * LEN[c]
             q = st[("f", c)][2]
-            nc.scalar.activation(out=st[("p4", c)][:, 2 * CW : 3 * CW], in_=q[:, 0:CW], func=ACT.Identity, scale=-3.0, bias=-2.0 / 3.0)
+            nc.scalar.activation(out=st[("p4", c)][:, 2 * cw : 3 * cw], in_=q[:, 0:cw], func=ACT.Identity, scale=-3.0, bias=-2.0 / 3.0)
 
-        def v_caff(c):
-            q = st[("f", c)][2]
-            nc.vector.tensor_scalar(
-                out=st[("p4", c)][:, 3 * CW : 4 * CW], in0=q[:, CW : 2 * CW], scalar1=3.0, scalar2=-2.0 / 3.0,
-                op0=ALU.mult, op1=ALU.add,
-            )
+        def caff(c):
+            cw = 512 * LEN[c]
+            dst = st[("p4", c)][:, 3 * cw : 4 * cw]
+            src = st[("f", c)][2][:, cw : 2 * cw]
+            if on_scalar(c):
+                nc.scalar.activation(out=dst, in_=src, func=ACT.Identity, scale=3.0, bias=-2.0 / 3.0)
+            else:
+                nc.vector.tensor_scalar(out=dst, in0=src, scalar1=3.0, scalar2=-2.0 / 3.0, op0=ALU.mult, op1=ALU.add)
 
         def v_s07(c):
-            s07 = b16p.tile([P, 2 * CW], BF16, align_bytes=64)
-            nc.vector.tensor_scalar(out=s07[:], in0=st[("p4", c)][:, 0 : 2 * CW], scalar1=0.0, scalar2=None, op0=ALU.max)
+            cw = 512 * LEN[c]
+            s07 = b16p.tile([P, 2 * cw], BF16, align_bytes=64)
+            nc.vector.tensor_scalar(out=s07[:], in0=st[("p4", c)][:, 0 : 2 * cw], scalar1=0.0, scalar2=None, op0=ALU.max)
             st[("s07", c)] = s07
 
         def v_masks(c):
+            cw = 512 * LEN[c]
             xg = st[("xg", c)]
-            mk = one.tile([P, 2 * CW], BF16)
-            nc.vector.tensor_scalar(out=mk[:, 0:CW], in0=xg[:], scalar1=0.2, scalar2=-1.0, op0=ALU.is_ge, op1=ALU.mult)
-            nc.vector.tensor_scalar(out=mk[:, CW : 2 * CW], in0=xg[:], scalar1=-0.2, scalar2=-1.0, op0=ALU.is_lt, op1=ALU.mult)
+            mk = one.tile([P, 2 * cw], BF16)
+            nc.vector.tensor_scalar(out=mk[:, 0:cw], in0=xg[:], scalar1=0.2, scalar2=-1.0, op0=ALU.is_ge, op1=ALU.mult)
+            nc.vector.tensor_scalar(out=mk[:, cw : 2 * cw], in0=xg[:], scalar1=-0.2, scalar2=-1.0, op0=ALU.is_lt, op1=ALU.mult)
             st[("mk", c)] = mk
 
         def quant(c, n0, n1, src):
             bc, bs = st[("b", c)]
-            nc.vector.quantize_mx(out=bc[:, n0 * WW : n1 * WW].bitcast(FP8X4), scales=bs[:, n0 * WW : n1 * WW], in_=src)
+            ww = P * LEN[c]
+            nc.vector.quantize_mx(out=bc[:, n0 * ww : n1 * ww].bitcast(FP8X4), scales=bs[:, n0 * ww : n1 * ww], in_=src)
 
         def v_qx(c):
-            bc = codep.tile([P, NV * WW], U32, align_bytes=64)
-            bs = codep.tile([P, NV * WW], U8, align_bytes=64)
+            ww = P * LEN[c]
+            bc = codep.tile([P, NV * ww], U32, align_bytes=64)
+            bs = codep.tile([P, NV * ww], U8, align_bytes=64)
             st[("b", c)] = (bc, bs)
             quant(c, XB, XB + 1, st[("xg", c)][:])
 
         def v_max(c):
-            w4 = one.tile([P, 4 * CW], BF16, align_bytes=64)
-            nc.vector.tensor_tensor(out=w4[:, 0 : 2 * CW], in0=st[("p4", c)][:, 2 * CW : 4 * CW], in1=st[("f", c)][1][:], op=ALU.max)
+            cw = 512 * LEN[c]
+            w4 = one.tile([P, 4 * cw], BF16, align_bytes=64)
+            nc.vector.tensor_tensor(out=w4[:, 0 : 2 * cw], in0=st[("p4", c)][:, 2 * cw : 4 * cw], in1=st[("f", c)][1][:], op=ALU.max)
             st[("w4", c)] = w4
 
         def v_min(c):
+            cw = 512 * LEN[c]
             w4 = st[("w4", c)]
-            nc.vector.tensor_tensor(out=w4[:, 0 : 2 * CW], in0=w4[:, 0 : 2 * CW], in1=st[("p4", c)][:, 0 : 2 * CW], op=ALU.min)
+            nc.vector.tensor_tensor(out=w4[:, 0 : 2 * cw], in0=w4[:, 0 : 2 * cw], in1=st[("p4", c)][:, 0 : 2 * cw], op=ALU.min)
 
         def v_mult(c):
+            cw = 512 * LEN[c]
             w4 = st[("w4", c)]
-            nc.vector.tensor_tensor(out=w4[:, 2 * CW : 4 * CW], in0=w4[:, 0 : 2 * CW], in1=st[("mk", c)][:], op=ALU.mult)
+            nc.vector.tensor_tensor(out=w4[:, 2 * cw : 4 * cw], in0=w4[:, 0 : 2 * cw], in1=st[("mk", c)][:], op=ALU.mult)
 
         def mm(c):
             bc, bs = st[("b", c)]
-            acc = ps_o.tile([P, TPC, O], F32)
-            for tl in range(TPC):
+            ww = P * LEN[c]
+            acc = ps_o.tile([P, LEN[c], O], F32)
+            for tl in range(LEN[c]):
                 for n, (v, w) in enumerate(PASSES):
-                    lo = v * WW + tl * P
+                    lo = v * ww + tl * P
                     nc.tensor.matmul_mx(
                         out=acc[:, tl, :],
                         lhsT=bc[:, lo : lo + P].bitcast(FP8X4),
@@ -238,32 +274,33 @@ def tile_kanlayer_t_kernel(tc, x, base_weight, spline_weight, out):
             st[("acc", c)] = acc
 
         def evac_out(c):
-            osb = outp.tile([P, TPC, O], F32)
+            osb = outp.tile([P, LEN[c], O], F32)
             nc.scalar.copy(out=osb[:], in_=st[("acc", c)][:])
-            nc.sync.dma_start(out=out_v[:, c * TPC : (c + 1) * TPC, :], in_=osb[:])
+            nc.sync.dma_start(out=out_v[:, T0[c] : T0[c] + LEN[c], :], in_=osb[:])
+
+        def on_scalar(c):
+            return 4 <= c < NCH - 2 and c % 2 == 0
 
         t_x(0)
-        s_copy(0)
-        s_front(0)
         t_x(1)
+        s_copy(0)
+        t_x(2)
+        s_front1(0)
         s_copy(1)
+        s_front2(0)
+        s_front3(0)
         for l in range(4):
-            w_reorder(l)
             w_transpose(l)
-        for l in range(4, 8):
-            w_reorder(l)
 
         for i in range(NCH + 1):
-            a, b = i < NCH, i >= 1
-            if i + 2 < NCH:
-                t_x(i + 2)
-            if i == 0:
-                for l in range(4):
-                    w_evac(l)
-            if i + 1 < NCH:
-                if i >= 1:
-                    s_copy(i + 1)
-                s_front(i + 1)
+            a, b, n = i < NCH, i >= 1, i + 1 < NCH
+            if i + 3 < NCH:
+                t_x(i + 3)
+            if n:
+                s_front1(i + 1)
+                if i + 2 < NCH:
+                    s_copy(i + 2)
+                s_front2(i + 1)
             if a:
                 v_ab(i)
             if b:
@@ -278,29 +315,42 @@ def tile_kanlayer_t_kernel(tc, x, base_weight, spline_weight, out):
                 v_mult(i - 1)
             if a:
                 v_s07(i)
-                v_caff(i)
                 s_daff(i)
+                if not on_scalar(i):
+                    caff(i)
+            if n:
+                s_front3(i + 1)
+            if a and on_scalar(i):
+                caff(i)
+            if i in (0, 2):
+                for l in range(3 * i, 3 * i + 3):
+                    w_evac(l)
+                for l in range(3 * i + 4, min(3 * i + 7, 9)):
+                    w_transpose(l)
             if b:
                 quant(i - 1, AN, CN + 1, st[("p4", i - 1)][:])
-            if i == 0:
-                for l in range(4, 8):
-                    w_transpose(l)
-                for l in range(4):
+            if 1 <= i < 4:
+                for l in range(3 * i - 3, 3 * i):
                     w_quant(l)
-                for l in range(4, 8):
-                    w_evac(l)
-                w_transpose(8)
-                w_evac(8)
-            if i == 1:
-                for l in range(4, 9):
-                    w_quant(l)
+            if i == 3:
+                mm(0)
+                mm(1)
+            if b:
+                quant(i - 1, W2, S1 + 1, st[("w4", i - 1)][:])
+                quant(i - 1, S0, S7 + 1, st[("s07", i - 1)][:])
             if a:
                 v_masks(i)
                 v_qx(i)
             if b:
-                quant(i - 1, W2, S1 + 1, st[("w4", i - 1)][:])
-                quant(i - 1, S0, S7 + 1, st[("s07", i - 1)][:])
-                mm(i - 1)
-            if i >= 2:
+                if i == 1:
+                    for l in range(3, 6):
+                        w_evac(l)
+                    for l in range(7, 9):
+                        w_transpose(l)
+                if i >= 3:
+                    mm(i - 1)
+                if i == 3:
+                    evac_out(0)
+            if i >= 3:
                 evac_out(i - 2)
         evac_out(NCH - 1)

@@ -25,14 +25,15 @@ R6 = 1.0 / math.sqrt(6.0)
 STEEP = 1024.0
 NV = 11
 AN, BN, DN, CN, W2, W1, S6, S1, S0, S7, XB = range(NV)
-NW = 13
-NEG = {2: 9, 4: 10, 3: 11, 5: 12}
+NW = 11
+NEG = {4: 9, 3: 10}
+TURNED = (2, 5)
 BASE = 8
 PASSES = [
     (XB, BASE),
     (AN, NEG[4]), (DN, NEG[4]), (BN, NEG[3]), (CN, NEG[3]),
-    (W2, 4), (W2, NEG[2]), (W1, 3), (W1, NEG[5]),
-    (S6, 6), (S6, NEG[2]), (S1, 1), (S1, NEG[5]),
+    (W2, 4), (W2, 2), (W1, 3), (W1, 5),
+    (S6, 6), (S6, 2), (S1, 1), (S1, 5),
     (S0, 0), (S0, 4), (S7, 7), (S7, 3),
 ]
 
@@ -112,8 +113,10 @@ def tile_kanlayer_t_kernel(tc, x, base_weight, spline_weight, out):
             if l < L:
                 dst = wg[:].rearrange("p (o t) -> p o t", t=4)
                 src = st[("wt", l)][:].rearrange("p t o -> p o t")
-                if 3 <= l < 6:
-                    nc.vector.tensor_copy(out=dst, in_=src)
+                if l in (0, 1, 3, 4, 5):
+                    nc.vector.tensor_scalar(out=dst, in0=src, scalar1=-1.0 if l in TURNED else 1.0, scalar2=None, op0=ALU.mult)
+                elif l in TURNED:
+                    nc.scalar.activation(out=dst, in_=src, func=ACT.Copy, scale=-1.0)
                 else:
                     nc.scalar.copy(out=dst, in_=src)
             else:
@@ -167,11 +170,8 @@ def tile_kanlayer_t_kernel(tc, x, base_weight, spline_weight, out):
             cw = 512 * LEN[c]
             d = st[("d", c)]
             f = f32p.tile([P, 2 * cw], F32)
-            m = mp.tile([P, 2 * cw], BF16)
             nc.scalar.activation(out=f[:], in_=d[:], func=ACT.Abs, scale=-1.0, bias=1.0)
-            nc.scalar.activation(out=m[:], in_=d[:], func=ACT.Identity, scale=-STEEP, bias=STEEP - 1.0 / 6.0)
             st[("a", c)] = f
-            st[("m", c)] = m
 
         def s_front3(c):
             cw = 512 * LEN[c]
@@ -180,34 +180,40 @@ def tile_kanlayer_t_kernel(tc, x, base_weight, spline_weight, out):
             u = f32p.tile([P, cw], F32)
             nc.scalar.activation(out=q[:], in_=f[:], func=ACT.Square, scale=R6, bias=-R6)
             nc.scalar.activation(out=u[:], in_=f[:, 0:cw], func=ACT.Abs, scale=-1.0, bias=1.0)
-            st[("f", c)] = (f, st[("m", c)], q, u)
+            st[("f", c)] = (f, q, u)
+
+        def s_ramp(c):
+            cw = 512 * LEN[c]
+            m = mp.tile([P, 2 * cw], BF16)
+            nc.scalar.activation(out=m[:], in_=st[("d", c)][:], func=ACT.Identity, scale=-STEEP, bias=STEEP - 1.0 / 6.0)
+            st[("m", c)] = m
 
         def v_ab(c):
             cw = 512 * LEN[c]
-            f, m, q, u = st[("f", c)]
+            f, q, u = st[("f", c)]
             p4 = b16p.tile([P, 4 * cw], BF16, align_bytes=64)
             nc.vector.scalar_tensor_tensor(out=p4[:, 0 : 2 * cw], in0=f[:], scalar=-1.0, in1=q[:], op0=ALU.add, op1=ALU.mult)
             st[("p4", c)] = p4
 
         def v_d(c):
             cw = 512 * LEN[c]
-            f, m, q, u = st[("f", c)]
+            f, q, u = st[("f", c)]
             nc.vector.scalar_tensor_tensor(out=q[:, 0:cw], in0=u[:], scalar=-2.0, in1=q[:, 0:cw], op0=ALU.add, op1=ALU.mult)
 
         def v_c(c):
             cw = 512 * LEN[c]
-            f, m, q, u = st[("f", c)]
+            f, q, u = st[("f", c)]
             nc.vector.scalar_tensor_tensor(out=q[:, cw : 2 * cw], in0=u[:], scalar=1.0, in1=q[:, cw : 2 * cw], op0=ALU.add, op1=ALU.mult)
 
         def s_daff(c):
             cw = 512 * LEN[c]
-            q = st[("f", c)][2]
+            q = st[("f", c)][1]
             nc.scalar.activation(out=st[("p4", c)][:, 2 * cw : 3 * cw], in_=q[:, 0:cw], func=ACT.Identity, scale=-3.0, bias=-2.0 / 3.0)
 
         def caff(c):
             cw = 512 * LEN[c]
             dst = st[("p4", c)][:, 3 * cw : 4 * cw]
-            src = st[("f", c)][2][:, cw : 2 * cw]
+            src = st[("f", c)][1][:, cw : 2 * cw]
             if on_scalar(c):
                 nc.scalar.activation(out=dst, in_=src, func=ACT.Identity, scale=3.0, bias=-2.0 / 3.0)
             else:
@@ -242,7 +248,7 @@ def tile_kanlayer_t_kernel(tc, x, base_weight, spline_weight, out):
         def v_max(c):
             cw = 512 * LEN[c]
             w4 = one.tile([P, 4 * cw], BF16, align_bytes=64)
-            nc.vector.tensor_tensor(out=w4[:, 0 : 2 * cw], in0=st[("p4", c)][:, 2 * cw : 4 * cw], in1=st[("f", c)][1][:], op=ALU.max)
+            nc.vector.tensor_tensor(out=w4[:, 0 : 2 * cw], in0=st[("p4", c)][:, 2 * cw : 4 * cw], in1=st[("m", c)][:], op=ALU.max)
             st[("w4", c)] = w4
 
         def v_min(c):
@@ -279,16 +285,19 @@ def tile_kanlayer_t_kernel(tc, x, base_weight, spline_weight, out):
             nc.sync.dma_start(out=out_v[:, T0[c] : T0[c] + LEN[c], :], in_=osb[:])
 
         def on_scalar(c):
-            return 4 <= c < NCH - 2 and c % 2 == 0
+            return 4 <= c < NCH - 2 and c % 4 != 1
 
         t_x(0)
         t_x(1)
         s_copy(0)
         t_x(2)
         s_front1(0)
-        s_copy(1)
+        v_masks(0)
+        v_qx(0)
         s_front2(0)
         s_front3(0)
+        s_ramp(0)
+        s_copy(1)
         for l in range(4):
             w_transpose(l)
 
@@ -322,11 +331,16 @@ def tile_kanlayer_t_kernel(tc, x, base_weight, spline_weight, out):
                 s_front3(i + 1)
             if a and on_scalar(i):
                 caff(i)
-            if i in (0, 2):
-                for l in range(3 * i, 3 * i + 3):
+            if n:
+                s_ramp(i + 1)
+            if i == 0:
+                for l in range(3):
                     w_evac(l)
-                for l in range(3 * i + 4, min(3 * i + 7, 9)):
+                for l in range(4, 7):
                     w_transpose(l)
+            if i == 2:
+                for l in range(6, 9):
+                    w_evac(l)
             if b:
                 quant(i - 1, AN, CN + 1, st[("p4", i - 1)][:])
             if 1 <= i < 4:
@@ -338,7 +352,7 @@ def tile_kanlayer_t_kernel(tc, x, base_weight, spline_weight, out):
             if b:
                 quant(i - 1, W2, S1 + 1, st[("w4", i - 1)][:])
                 quant(i - 1, S0, S7 + 1, st[("s07", i - 1)][:])
-            if a:
+            if 0 < i < NCH:
                 v_masks(i)
                 v_qx(i)
             if b:

@@ -222,7 +222,10 @@ def tile_kanlayer_t_kernel(tc, x, base_weight, spline_weight, out):
         def v_s07(c):
             cw = 512 * LEN[c]
             s07 = b16p.tile([P, 2 * cw], BF16, align_bytes=64)
-            nc.vector.tensor_scalar(out=s07[:], in0=st[("p4", c)][:, 0 : 2 * cw], scalar1=0.0, scalar2=None, op0=ALU.max)
+            if c >= NCH - 2:
+                nc.scalar.activation(out=s07[:], in_=st[("p4", c)][:, 0 : 2 * cw], func=ACT.Relu)
+            else:
+                nc.vector.tensor_scalar(out=s07[:], in0=st[("p4", c)][:, 0 : 2 * cw], scalar1=0.0, scalar2=None, op0=ALU.max)
             st[("s07", c)] = s07
 
         def v_masks(c):
@@ -285,7 +288,7 @@ def tile_kanlayer_t_kernel(tc, x, base_weight, spline_weight, out):
             nc.sync.dma_start(out=out_v[:, T0[c] : T0[c] + LEN[c], :], in_=osb[:])
 
         def on_scalar(c):
-            return 4 <= c < NCH - 2 and c % 4 != 1
+            return c >= NCH - 2 or (c >= 4 and c % 4 != 1)
 
         t_x(0)
         t_x(1)
@@ -323,7 +326,8 @@ def tile_kanlayer_t_kernel(tc, x, base_weight, spline_weight, out):
             if b:
                 v_mult(i - 1)
             if a:
-                v_s07(i)
+                if i < NCH - 2:
+                    v_s07(i)
                 s_daff(i)
                 if not on_scalar(i):
                     caff(i)
@@ -333,6 +337,8 @@ def tile_kanlayer_t_kernel(tc, x, base_weight, spline_weight, out):
                 caff(i)
             if n:
                 s_ramp(i + 1)
+            if NCH - 2 <= i < NCH:
+                v_s07(i)
             if i == 0:
                 for l in range(3):
                     w_evac(l)

@@ -163,14 +163,16 @@ def tile_kanlayer_t_kernel(tc, x, base_weight, spline_weight, out):
             xg = st[("xg", c)]
             d = one.tile([P, 2 * cw], F32)
             nc.scalar.activation(out=d[:, 0:cw], in_=xg[:], func=ACT.Abs, scale=2.5, bias=-0.5)
-            nc.scalar.activation(out=d[:, cw : 2 * cw], in_=xg[:], func=ACT.Abs, scale=2.5, bias=0.5)
+            if c > 0:
+                nc.scalar.activation(out=d[:, cw : 2 * cw], in_=xg[:], func=ACT.Abs, scale=2.5, bias=0.5)
             st[("d", c)] = d
 
         def s_front2(c):
             cw = 512 * LEN[c]
             d = st[("d", c)]
             f = f32p.tile([P, 2 * cw], F32)
-            nc.scalar.activation(out=f[:], in_=d[:], func=ACT.Abs, scale=-1.0, bias=1.0)
+            w = cw if c == 0 else 2 * cw
+            nc.scalar.activation(out=f[:, 0:w], in_=d[:, 0:w], func=ACT.Abs, scale=-1.0, bias=1.0)
             st[("a", c)] = f
 
         def s_front3(c):
@@ -178,7 +180,8 @@ def tile_kanlayer_t_kernel(tc, x, base_weight, spline_weight, out):
             f = st[("a", c)]
             q = f32p.tile([P, 2 * cw], F32)
             u = f32p.tile([P, cw], F32)
-            nc.scalar.activation(out=q[:], in_=f[:], func=ACT.Square, scale=R6, bias=-R6)
+            w = cw if c == 0 else 2 * cw
+            nc.scalar.activation(out=q[:, 0:w], in_=f[:, 0:w], func=ACT.Square, scale=R6, bias=-R6)
             nc.scalar.activation(out=u[:], in_=f[:, 0:cw], func=ACT.Abs, scale=-1.0, bias=1.0)
             st[("f", c)] = (f, q, u)
 
@@ -187,6 +190,23 @@ def tile_kanlayer_t_kernel(tc, x, base_weight, spline_weight, out):
             m = mp.tile([P, 2 * cw], BF16)
             nc.scalar.activation(out=m[:], in_=st[("d", c)][:], func=ACT.Identity, scale=-STEEP, bias=STEEP - 1.0 / 6.0)
             st[("m", c)] = m
+
+        def v_affine(out, in_, scale, bias):
+            nc.vector.tensor_scalar(out=out, in0=in_, scalar1=scale, scalar2=bias, op0=ALU.mult, op1=ALU.add)
+
+        def v_first_half():
+            cw = 512 * LEN[0]
+            half = slice(cw, 2 * cw)
+            d, (f, q, u) = st[("d", 0)][:, half], st[("f", 0)]
+            y = one.tile([P, cw], F32)
+            v_affine(y[:], st[("xg", 0)][:], 2.5, 0.5)
+            nc.vector.scalar_tensor_tensor(out=d, in0=y[:], scalar=-1.0, in1=y[:], op0=ALU.mult, op1=ALU.max)
+            z = one.tile([P, cw], F32)
+            v_affine(z[:], d, 1.0, -1.0)
+            nc.vector.scalar_tensor_tensor(out=f[:, half], in0=z[:], scalar=-1.0, in1=z[:], op0=ALU.mult, op1=ALU.max)
+            g = one.tile([P, cw], F32)
+            v_affine(g[:], f[:, half], 1.0, -1.0)
+            nc.vector.scalar_tensor_tensor(out=q[:, half], in0=g[:], scalar=1.0 / 6.0, in1=g[:], op0=ALU.mult, op1=ALU.mult)
 
         def v_ab(c):
             cw = 512 * LEN[c]
@@ -288,17 +308,18 @@ def tile_kanlayer_t_kernel(tc, x, base_weight, spline_weight, out):
             nc.sync.dma_start(out=out_v[:, T0[c] : T0[c] + LEN[c], :], in_=osb[:])
 
         def on_scalar(c):
-            return c >= NCH - 2 or (c >= 4 and c % 4 != 1)
+            return c >= NCH - 2 or (c >= 4 and c % 3 != 1)
 
         t_x(0)
         t_x(1)
         s_copy(0)
         t_x(2)
         s_front1(0)
-        v_masks(0)
-        v_qx(0)
         s_front2(0)
         s_front3(0)
+        v_first_half()
+        v_masks(0)
+        v_qx(0)
         s_ramp(0)
         s_copy(1)
         for l in range(4):

@@ -308,7 +308,7 @@ def tile_kanlayer_t_kernel(tc, x, base_weight, spline_weight, out):
             nc.sync.dma_start(out=out_v[:, T0[c] : T0[c] + LEN[c], :], in_=osb[:])
 
         def on_scalar(c):
-            return c >= NCH - 2 or (c >= 4 and c % 3 != 1)
+            return c >= NCH - 2 or (c >= 4 and c % 2 == 0)
 
         t_x(0)
         t_x(1)

from contextlib import ExitStack
import math

import concourse.bass as bass
import concourse.mybir as mybir
import concourse.tile as tile
from concourse.masks import make_identity

F32 = mybir.dt.float32
BF16 = mybir.dt.bfloat16
U32 = mybir.dt.uint32
U8 = mybir.dt.uint8
FP8X4 = mybir.dt.float8_e4m3fn_x4
ALU = mybir.AluOpType
ACT = mybir.ActivationFunctionType

P = 128
B, I, O, L = 4096, 512, 256, 8
NT = B // P
LEN = [1, 1] + [2] * 14 + [1, 1]
NCH = len(LEN)
T0 = [sum(LEN[:c]) for c in range(NCH)]
FLOPS = 2 * B * O * (I + I * L)
R6 = 1.0 / math.sqrt(6.0)
STEEP = 1024.0
NV = 11
AN, BN, DN, CN, W2, W1, S6, S1, S0, S7, XB = range(NV)
NW = 11
NEG = {4: 9, 3: 10}
TURNED = (2, 5)
BASE = 8
PASSES = [
    (XB, BASE),
    (AN, NEG[4]), (DN, NEG[4]), (BN, NEG[3]), (CN, NEG[3]),
    (W2, 4), (W2, 2), (W1, 3), (W1, 5),
    (S6, 6), (S6, 2), (S1, 1), (S1, 5),
    (S0, 0), (S0, 4), (S7, 7), (S7, 3),
]


def tile_kanlayer_t_kernel(tc, x, base_weight, spline_weight, out):
    nc = tc.nc
    with ExitStack() as ctx:
        const = ctx.enter_context(tc.tile_pool(name="const", bufs=1))
        wgp = ctx.enter_context(tc.tile_pool(name="wgp", bufs=5))
        wnp = ctx.enter_context(tc.tile_pool(name="wnp", bufs=2))
        xgp = ctx.enter_context(tc.tile_pool(name="xgp", bufs=3))
        f32p = ctx.enter_context(tc.tile_pool(name="f32p", bufs=2))
        mp = ctx.enter_context(tc.tile_pool(name="mp", bufs=3))
        one = ctx.enter_context(tc.tile_pool(name="one", bufs=1))
        b16p = ctx.enter_context(tc.tile_pool(name="b16p", bufs=2))
        codep = ctx.enter_context(tc.tile_pool(name="codep", bufs=3))
        outp = ctx.enter_context(tc.tile_pool(name="outp", bufs=2))
        ps_x = ctx.enter_context(tc.psum_pool(name="ps_x", bufs=2))
        ps_w = ctx.enter_context(tc.psum_pool(name="ps_w", bufs=4))
        ps_o = ctx.enter_context(tc.psum_pool(name="ps_o", bufs=2))
        ctx.enter_context(tc.manual_schedule())

        ident = const.tile([P, P], F32)
        make_identity(nc, ident[:])
        identb = const.tile([P, P], BF16)
        make_identity(nc, identb[:])
        x_sb = const.tile([P, NT * I], BF16)
        sw_sb = const.tile([P, 2 * I * L], BF16)
        bw_sb = const.tile([P, 2 * I], BF16)
        wc = const.tile([P, NW * O], U32, align_bytes=64)
        ws = const.tile([P, NW * O], U8, align_bytes=64)

        x_v = x.rearrange("(p t) i -> p t i", t=NT)
        x_t = x_sb[:].rearrange("p (t i) -> p t i", i=I)
        out_v = out.rearrange("(p t) o -> p t o", t=NT)

        def load_x(t0, t1):
            nc.sync.dma_start(out=x_t[:, t0:t1, :], in_=x_v[:, t0:t1, :])

        load_x(0, 1)
        load_x(1, 4)
        nc.sync.dma_start(
            out=sw_sb[:].rearrange("p (a k) -> p a k", a=2),
            in_=spline_weight.rearrange("(a p) i l -> p a (i l)", p=P),
        )
        nc.sync.dma_start(
            out=bw_sb[:].rearrange("p (a k) -> p a k", a=2),
            in_=base_weight.rearrange("(a p) i -> p a i", p=P),
        )
        for j in range(1, 8):
            load_x(4 * j, 4 * j + 4)

        x_w = x_sb[:].bitcast(F32)
        st = {}

        sw_v = sw_sb[:].rearrange("p (a u k e l) -> p a l u e k", a=2, u=2, e=2, l=L)

        def w_transpose(l):
            if l < L:
                wt = ps_w.tile([P, 4, O], BF16)
                for a in range(2):
                    for t in range(4):
                        nc.tensor.transpose(wt[:, t, a * P : (a + 1) * P], sw_v[:, a, l, t // 2, t % 2], identb[:])
            else:
                wt = ps_w.tile([P, 2, O], F32)
                for a in range(2):
                    for u in range(2):
                        nc.tensor.transpose(
                            wt[:, u, a * P : (a + 1) * P],
                            bw_sb[:].bitcast(F32)[:, a * 256 + u * P : a * 256 + (u + 1) * P],
                            ident[:],
                        )
            st[("wt", l)] = wt

        def w_evac(l):
            wg = wgp.tile([P, 4 * O], BF16, align_bytes=64)
            if l < L:
                dst = wg[:].rearrange("p (o t) -> p o t", t=4)
                src = st[("wt", l)][:].rearrange("p t o -> p o t")
                if l in (0, 1, 3, 4, 5):
                    nc.vector.tensor_scalar(out=dst, in0=src, scalar1=-1.0 if l in TURNED else 1.0, scalar2=None, op0=ALU.mult)
                elif l in TURNED:
                    nc.scalar.activation(out=dst, in_=src, func=ACT.Copy, scale=-1.0)
                else:
                    nc.scalar.copy(out=dst, in_=src)
            else:
                nc.scalar.copy(
                    out=wg[:].bitcast(F32).rearrange("p (o u) -> p o u", u=2),
                    in_=st[("wt", l)][:].rearrange("p u o -> p o u"),
                )
            st[("wg", l)] = wg

        def w_quant_into(n, wg):
            nc.vector.quantize_mx(
                out=wc[:, n * O : (n + 1) * O].bitcast(FP8X4), scales=ws[:, n * O : (n + 1) * O], in_=wg[:]
            )

        def w_quant(l):
            wg = st[("wg", l)]
            w_quant_into(l, wg)
            if l in NEG:
                wn = wnp.tile([P, 4 * O], BF16, align_bytes=64)
                nc.vector.tensor_scalar(out=wn[:], in0=wg[:], scalar1=-1.0, scalar2=None, op0=ALU.mult)
                w_quant_into(NEG[l], wn)

        def t_x(c):
            xt = ps_x.tile([P, LEN[c], 2, P], F32)
            for tl in range(LEN[c]):
                t = T0[c] + tl
                for u in range(2):
                    nc.tensor.transpose(
                        xt[:, tl, u, :], x_w[:, t * 256 + u * P : t * 256 + (u + 1) * P], ident[:]
                    )
            st[("xt", c)] = xt

        def s_copy(c):
            cw = 512 * LEN[c]
            xg = xgp.tile([P, cw], BF16, align_bytes=64)
            nc.scalar.copy(
                out=xg[:].bitcast(F32).rearrange("p (t m u) -> p t m u", t=LEN[c], u=2),
                in_=st[("xt", c)][:].rearrange("p t u m -> p t m u"),
            )
            st[("xg", c)] = xg

        def s_front1(c):
            cw = 512 * LEN[c]
            xg = st[("xg", c)]
            d = one.tile([P, 2 * cw], F32)
            nc.scalar.activation(out=d[:, 0:cw], in_=xg[:], func=ACT.Abs, scale=2.5, bias=-0.5)
            if c > 0:
                nc.scalar.activation(out=d[:, cw : 2 * cw], in_=xg[:], func=ACT.Abs, scale=2.5, bias=0.5)
            st[("d", c)] = d

        def s_front2(c):
            cw = 512 * LEN[c]
            d = st[("d", c)]
            f = f32p.tile([P, 2 * cw], F32)
            w = cw if c == 0 else 2 * cw
            nc.scalar.activation(out=f[:, 0:w], in_=d[:, 0:w], func=ACT.Abs, scale=-1.0, bias=1.0)
            st[("a", c)] = f

        def s_front3(c):
            cw = 512 * LEN[c]
            f = st[("a", c)]
            q = f32p.tile([P, 2 * cw], F32)
            u = f32p.tile([P, cw], F32)
            w = cw if c == 0 else 2 * cw
            nc.scalar.activation(out=q[:, 0:w], in_=f[:, 0:w], func=ACT.Square, scale=R6, bias=-R6)
            nc.scalar.activation(out=u[:], in_=f[:, 0:cw], func=ACT.Abs, scale=-1.0, bias=1.0)
            st[("f", c)] = (f, q, u)

        def s_ramp(c):
            cw = 512 * LEN[c]
            m = mp.tile([P, 2 * cw], BF16)
            nc.scalar.activation(out=m[:], in_=st[("d", c)][:], func=ACT.Identity, scale=-STEEP, bias=STEEP - 1.0 / 6.0)
            st[("m", c)] = m

        def v_affine(out, in_, scale, bias):
            nc.vector.tensor_scalar(out=out, in0=in_, scalar1=scale, scalar2=bias, op0=ALU.mult, op1=ALU.add)

        def v_first_half():
            cw = 512 * LEN[0]
            half = slice(cw, 2 * cw)
            d, (f, q, u) = st[("d", 0)][:, half], st[("f", 0)]
            y = one.tile([P, cw], F32)
            v_affine(y[:], st[("xg", 0)][:], 2.5, 0.5)
            nc.vector.scalar_tensor_tensor(out=d, in0=y[:], scalar=-1.0, in1=y[:], op0=ALU.mult, op1=ALU.max)
            z = one.tile([P, cw], F32)
            v_affine(z[:], d, 1.0, -1.0)
            nc.vector.scalar_tensor_tensor(out=f[:, half], in0=z[:], scalar=-1.0, in1=z[:], op0=ALU.mult, op1=ALU.max)
            g = one.tile([P, cw], F32)
            v_affine(g[:], f[:, half], 1.0, -1.0)
            nc.vector.scalar_tensor_tensor(out=q[:, half], in0=g[:], scalar=1.0 / 6.0, in1=g[:], op0=ALU.mult, op1=ALU.mult)

        def v_ab(c):
            cw = 512 * LEN[c]
            f, q, u = st[("f", c)]
            p4 = b16p.tile([P, 4 * cw], BF16, align_bytes=64)
            nc.vector.scalar_tensor_tensor(out=p4[:, 0 : 2 * cw], in0=f[:], scalar=-1.0, in1=q[:], op0=ALU.add, op1=ALU.mult)
            st[("p4", c)] = p4

        def v_d(c):
            cw = 512 * LEN[c]
            f, q, u = st[("f", c)]
            nc.vector.scalar_tensor_tensor(out=q[:, 0:cw], in0=u[:], scalar=-2.0, in1=q[:, 0:cw], op0=ALU.add, op1=ALU.mult)

        def v_c(c):
            cw = 512 * LEN[c]
            f, q, u = st[("f", c)]
            nc.vector.scalar_tensor_tensor(out=q[:, cw : 2 * cw], in0=u[:], scalar=1.0, in1=q[:, cw : 2 * cw], op0=ALU.add, op1=ALU.mult)

        def s_daff(c):
            cw = 512 * LEN[c]
            q = st[("f", c)][1]
            nc.scalar.activation(out=st[("p4", c)][:, 2 * cw : 3 * cw], in_=q[:, 0:cw], func=ACT.Identity, scale=-3.0, bias=-2.0 / 3.0)

        def caff(c):
            cw = 512 * LEN[c]
            dst = st[("p4", c)][:, 3 * cw : 4 * cw]
            src = st[("f", c)][1][:, cw : 2 * cw]
            if on_scalar(c):
                nc.scalar.activation(out=dst, in_=src, func=ACT.Identity, scale=3.0, bias=-2.0 / 3.0)
            else:
                nc.vector.tensor_scalar(out=dst, in0=src, scalar1=3.0, scalar2=-2.0 / 3.0, op0=ALU.mult, op1=ALU.add)

        def v_s07(c):
            cw = 512 * LEN[c]
            s07 = b16p.tile([P, 2 * cw], BF16, align_bytes=64)
            if c >= NCH - 2:
                nc.scalar.activation(out=s07[:], in_=st[("p4", c)][:, 0 : 2 * cw], func=ACT.Relu)
            else:
                nc.vector.tensor_scalar(out=s07[:], in0=st[("p4", c)][:, 0 : 2 * cw], scalar1=0.0, scalar2=None, op0=ALU.max)
            st[("s07", c)] = s07

        def v_masks(c):
            cw = 512 * LEN[c]
            xg = st[("xg", c)]
            mk = one.tile([P, 2 * cw], BF16)
            nc.vector.tensor_scalar(out=mk[:, 0:cw], in0=xg[:], scalar1=0.2, scalar2=-1.0, op0=ALU.is_ge, op1=ALU.mult)
            nc.vector.tensor_scalar(out=mk[:, cw : 2 * cw], in0=xg[:], scalar1=-0.2, scalar2=-1.0, op0=ALU.is_lt, op1=ALU.mult)
            st[("mk", c)] = mk

        def quant(c, n0, n1, src):
            bc, bs = st[("b", c)]
            ww = P * LEN[c]
            nc.vector.quantize_mx(out=bc[:, n0 * ww : n1 * ww].bitcast(FP8X4), scales=bs[:, n0 * ww : n1 * ww], in_=src)

        def v_qx(c):
            ww = P * LEN[c]
            bc = codep.tile([P, NV * ww], U32, align_bytes=64)
            bs = codep.tile([P, NV * ww], U8, align_bytes=64)
            st[("b", c)] = (bc, bs)
            quant(c, XB, XB + 1, st[("xg", c)][:])

        def v_max(c):
            cw = 512 * LEN[c]
            w4 = one.tile([P, 4 * cw], BF16, align_bytes=64)
            nc.vector.tensor_tensor(out=w4[:, 0 : 2 * cw], in0=st[("p4", c)][:, 2 * cw : 4 * cw], in1=st[("m", c)][:], op=ALU.max)
            st[("w4", c)] = w4

        def v_min(c):
            cw = 512 * LEN[c]
            w4 = st[("w4", c)]
            nc.vector.tensor_tensor(out=w4[:, 0 : 2 * cw], in0=w4[:, 0 : 2 * cw], in1=st[("p4", c)][:, 0 : 2 * cw], op=ALU.min)

        def v_mult(c):
            cw = 512 * LEN[c]
            w4 = st[("w4", c)]
            nc.vector.tensor_tensor(out=w4[:, 2 * cw : 4 * cw], in0=w4[:, 0 : 2 * cw], in1=st[("mk", c)][:], op=ALU.mult)

        def mm(c):
            bc, bs = st[("b", c)]
            ww = P * LEN[c]
            acc = ps_o.tile([P, LEN[c], O], F32)
            for tl in range(LEN[c]):
                for n, (v, w) in enumerate(PASSES):
                    lo = v * ww + tl * P
                    nc.tensor.matmul_mx(
                        out=acc[:, tl, :],
                        lhsT=bc[:, lo : lo + P].bitcast(FP8X4),
                        lhsT_scale=bs[:, lo : lo + P],
                        rhs=wc[:, w * O : (w + 1) * O].bitcast(FP8X4),
                        rhs_scale=ws[:, w * O : (w + 1) * O],
                        start=(n == 0),
                        stop=(n == len(PASSES) - 1),
                    )
            st[("acc", c)] = acc

        def evac_out(c):
            osb = outp.tile([P, LEN[c], O], F32)
            nc.scalar.copy(out=osb[:], in_=st[("acc", c)][:])
            nc.sync.dma_start(out=out_v[:, T0[c] : T0[c] + LEN[c], :], in_=osb[:])

        def on_scalar(c):
            return c >= NCH - 2 or (c >= 4 and c % 2 == 0)

        t_x(0)
        t_x(1)
        s_copy(0)
        t_x(2)
        s_front1(0)
        s_front2(0)
        s_front3(0)
        v_first_half()
        v_masks(0)
        v_qx(0)
        s_ramp(0)
        s_copy(1)
        for l in range(4):
            w_transpose(l)

        for i in range(NCH + 1):
            a, b, n = i < NCH, i >= 1, i + 1 < NCH
            if i + 3 < NCH:
                t_x(i + 3)
            if n:
                s_front1(i + 1)
                if i + 2 < NCH:
                    s_copy(i + 2)
                s_front2(i + 1)
            if a:
                v_ab(i)
            if b:
                v_max(i - 1)
            if a:
                v_d(i)
            if b:
                v_min(i - 1)
            if a:
                v_c(i)
            if b:
                v_mult(i - 1)
            if a:
                if i < NCH - 2:
                    v_s07(i)
                s_daff(i)
                if not on_scalar(i):
                    caff(i)
            if n:
                s_front3(i + 1)
            if a and on_scalar(i):
                caff(i)
            if n:
                s_ramp(i + 1)
            if NCH - 2 <= i < NCH:
                v_s07(i)
            if i == 0:
                for l in range(3):
                    w_evac(l)
                for l in range(4, 7):
                    w_transpose(l)
            if i == 2:
                for l in range(6, 9):
                    w_evac(l)
            if b:
                quant(i - 1, AN, CN + 1, st[("p4", i - 1)][:])
            if 1 <= i < 4:
                for l in range(3 * i - 3, 3 * i):
                    w_quant(l)
            if i == 3:
                mm(0)
                mm(1)
            if b:
                quant(i - 1, W2, S1 + 1, st[("w4", i - 1)][:])
                quant(i - 1, S0, S7 + 1, st[("s07", i - 1)][:])
            if 0 < i < NCH:
                v_masks(i)
                v_qx(i)
            if b:
                if i == 1:
                    for l in range(3, 6):
                        w_evac(l)
                    for l in range(7, 9):
                        w_transpose(l)
                if i >= 3:
                    mm(i - 1)
                if i == 3:
                    evac_out(0)
            if i >= 3:
                evac_out(i - 2)
        evac_out(NCH - 1)
